import numpy as np
import ml_dtypes


def mxq(x, axis, fmt="e4m3"):
    dtype, down = {"e4m3": (ml_dtypes.float8_e4m3fn, 7), "e5m2": (ml_dtypes.float8_e5m2, 14)}[fmt]
    v = np.moveaxis(np.asarray(x, np.float32).astype(ml_dtypes.bfloat16).astype(np.float64), axis, -1)
    blocks = v.reshape(v.shape[:-1] + (-1, 32))
    amax = np.abs(blocks).max(-1, keepdims=True)
    byte = np.maximum(np.where(amax > 0, np.frexp(amax)[1] - 1 + 127, 0) - down, 1)
    scale = np.exp2(byte - 127.0)
    codes = (blocks / scale).astype(np.float32).astype(dtype).astype(np.float64)
    return np.moveaxis((codes * scale).reshape(v.shape), -1, axis)


WIDE = False


def mx_kscale(k):
    if not WIDE:
        return np.ones(k)
    levels = np.array([10, -10, 5, -5, 0])
    if k % 512:
        return np.exp2(np.random.permutation(np.resize(levels, k // 32))).repeat(32)
    a = np.empty((k // 512, 16))
    for p in range(k // 512):
        a[p, :8] = np.random.permutation(np.resize(levels, 8))
        for g in range(8):
            far = levels[np.abs(levels - a[p, g]) >= 10]
            a[p, g + 8] = far[np.random.randint(len(far))]
    return np.exp2(a.ravel()).repeat(32)


BF16 = ml_dtypes.bfloat16


def bf(x):
    return np.asarray(x, np.float32).astype(BF16)


def f64(x):
    return np.asarray(x).astype(np.float64)


S, D, N_HEADS, N_KV_HEADS, HEAD_DIM = 512, 2048, 16, 4, 128
Q_DIM = N_HEADS * HEAD_DIM
KV_DIM = N_KV_HEADS * HEAD_DIM
ROPE_THETA = 500000.0


def apply_rope(t, cos, sin):
    te = t[:, :, ::2]
    to = t[:, :, 1::2]
    c = cos[:, None, :]
    s = sin[:, None, :]
    te_rot = te * c - to * s
    to_rot = te * s + to * c
    return np.stack([te_rot, to_rot], axis=-1).reshape(t.shape)


def draw0():
    s = mx_kscale(D)
    inv_freq = 1.0 / ROPE_THETA ** (np.arange(0, HEAD_DIM, 2) / HEAD_DIM)
    angles = np.arange(S)[:, None] * inv_freq[None, :]
    return {"x": bf(np.random.standard_normal((S, D)) * s),
            "freqs_cos": bf(np.cos(angles)),
            "freqs_sin": bf(np.sin(angles)),
            "wqkv": bf(np.random.standard_normal((Q_DIM + 2 * KV_DIM, D)) / np.sqrt(D) / s[None, :])}


def core(x, freqs_cos, freqs_sin, wqkv):
    qkv = mxq(f64(x), 1, "e4m3") @ mxq(f64(wqkv), 1, "e4m3").T
    q = qkv[:, :Q_DIM].reshape(S, N_HEADS, HEAD_DIM)
    k = qkv[:, Q_DIM:Q_DIM + KV_DIM].reshape(S, N_KV_HEADS, HEAD_DIM)
    v = qkv[:, Q_DIM + KV_DIM:].reshape(S, N_KV_HEADS, HEAD_DIM)
    cos, sin = f64(freqs_cos), f64(freqs_sin)
    return apply_rope(q, cos, sin), apply_rope(k, cos, sin), v


def e4m3fn_bytes(y):
    return np.clip(np.asarray(y, np.float64), -448.0, 448.0).astype(np.float32).astype(ml_dtypes.float8_e4m3fn).view(np.uint8)


def e4m3fn_values(b):
    return np.asarray(b, np.uint8).view(ml_dtypes.float8_e4m3fn).astype(np.float64)


def setup_inputs():
    d = draw0()
    x0 = np.asarray(d['wqkv']).astype(np.float64)
    s = (np.max(np.abs(x0), axis=(0,), keepdims=True) / 448.0).astype(np.float32)
    out = {}
    for k, v in d.items():
        if k == 'wqkv':
            out['wqkv_bytes'] = e4m3fn_bytes(x0 / s.astype(np.float64))
            out['wqkv_scale'] = s
        else:
            out[k] = v
    return out


def reference(x, freqs_cos, freqs_sin, wqkv_bytes, wqkv_scale):
    return core(x, freqs_cos, freqs_sin, e4m3fn_values(wqkv_bytes) * wqkv_scale.astype(np.float64))

@@ -1,0 +1,255 @@
+from contextlib import ExitStack
+
+import concourse.mybir as mybir
+from concourse.masks import make_identity
+
+S, D = 512, 2048
+FLOPS = 2 * 512 * 3072 * 2048
+
+F32 = mybir.dt.float32
+BF16 = mybir.dt.bfloat16
+U32 = mybir.dt.uint32
+U8 = mybir.dt.uint8
+FP8 = mybir.dt.float8_e4m3fn
+FP8X4 = mybir.dt.float8_e4m3fn_x4
+MULT = mybir.AluOpType.mult
+ADD = mybir.AluOpType.add
+
+P = 128
+NG = 4
+NT = 6
+ADD_ON_GPSIMD = True
+G_UNITS = ((0, 0), (0, 1))
+
+
+def tile_mha_pa_kernel(tc, x, freqs_cos, freqs_sin, wqkv_bytes, wqkv_scale, out_0, out_1, out_2):
+    nc = tc.nc
+    with ExitStack() as ctx:
+        const = ctx.enter_context(tc.tile_pool(name="const", bufs=1))
+        wbp = ctx.enter_context(tc.tile_pool(name="wbp", bufs=24))
+        xp = ctx.enter_context(tc.tile_pool(name="xp", bufs=8))
+        wfp = ctx.enter_context(tc.tile_pool(name="wfp", bufs=8))
+        grp = ctx.enter_context(tc.tile_pool(name="grp", bufs=2))
+        tmpp = ctx.enter_context(tc.tile_pool(name="tmpp", bufs=3))
+        wcp = ctx.enter_context(tc.tile_pool(name="wcp", bufs=3))
+        prp = ctx.enter_context(tc.tile_pool(name="prp", bufs=4))
+        op = ctx.enter_context(tc.tile_pool(name="op", bufs=4))
+        ptp = ctx.enter_context(tc.psum_pool(name="ptp", bufs=4))
+        accp = ctx.enter_context(tc.psum_pool(name="accp", bufs=4))
+
+        ident = const.tile([P, P], F32, name="ident", tag="ident")
+        make_identity(nc, ident[:])
+
+        sc = const.tile([P, NG, 1, 2, 2], F32, name="sc", tag="sc")
+        nc.gpsimd.dma_start(
+            out=sc[:, :, 0, :, :],
+            in_=wqkv_scale.rearrange("o (g p u e) -> p (o g) u e", p=P, u=2, e=2),
+        )
+        cosb = const.tile([P, 4, 1, 64], BF16, name="cosb", tag="cosb")
+        sinb = const.tile([P, 4, 1, 64], BF16, name="sinb", tag="sinb")
+        nc.sync.dma_start(out=cosb[:, :, 0, :], in_=freqs_cos.rearrange("(m p) i -> p m i", p=P))
+        nc.sync.dma_start(out=sinb[:, :, 0, :], in_=freqs_sin.rearrange("(m p) i -> p m i", p=P))
+
+        w_par = wqkv_bytes.rearrange("(j q) k -> q j k", q=2)
+
+        def w_rows(t, a):
+            if t < 5:
+                return w_par[a // 2, 256 * t + 128 * (a % 2) : 256 * t + 128 * (a % 2) + 128, :]
+            return wqkv_bytes[2560 + 128 * a : 2560 + 128 * a + 128, :]
+
+        wbytes = {}
+
+        def load_w(t, a):
+            wb = wbp.tile([P, D], U8, name="wbytes", tag="wbytes")
+            nc.sync.dma_start(out=wb[:], in_=w_rows(t, a))
+            wbytes[(t, a)] = wb
+
+        xs = {}
+        x_pairs = x.rearrange("(r m p) k -> r p m k", m=2, p=P)
+
+        def load_x(pr, g):
+            xt = xp.tile([P, 2, 512], BF16, name="xs", tag="xs")
+            nc.sync.dma_start(out=xt[:], in_=x_pairs[pr, :, :, 512 * g : 512 * g + 512])
+            xs[(pr, g)] = xt
+
+        for g in range(NG):
+            load_x(0, g)
+        load_w(0, 0)
+        load_w(0, 1)
+        for g in range(NG):
+            load_x(1, g)
+        load_w(0, 2)
+        load_w(0, 3)
+        for t in range(1, NT):
+            for a in range(4):
+                load_w(t, a)
+
+        tab = const.tile([P, 4, 2, 512], F32, name="tab", tag="tab")
+        for q, f, src, sign in ((0, 0, cosb, 1.0), (0, 1, sinb, -1.0), (1, 0, sinb, 1.0), (1, 1, cosb, 1.0)):
+            nc.gpsimd.tensor_scalar(
+                out=tab[:, :, q, 256 * f : 256 * f + 256].rearrange("p m (h i) -> p m h i", h=4),
+                in0=src[:].to_broadcast([P, 4, 4, 64]),
+                scalar1=sign,
+                scalar2=0.0,
+                op0=MULT,
+                op1=ADD,
+            )
+
+        def transposes(pt, words, w0):
+            for u in range(2):
+                for b in range(2):
+                    nc.tensor.transpose(
+                        out=pt[:, u, 128 * b : 128 * b + 128],
+                        in_=words[b][:, w0 + u : w0 + 256 : 2],
+                        identity=ident[:],
+                    )
+
+        def words_out(dst, pr):
+            return (
+                dst
+                .rearrange("p r t -> p (r t)")[:, 1024 * pr : 1024 * pr + 1024]
+                .bitcast(F32)
+                .rearrange("p (r u) -> p r u", u=2)
+            )
+
+        xc = const.tile([P, NG, S], U32, name="xc", tag="xc", align_bytes=64)
+        xsc = const.tile([P, NG, S], U8, name="xsc", tag="xsc", align_bytes=64)
+        xg = []
+        for h in range(2):
+            xgt = grp.tile([P, 2, 512, 4], BF16, name="gr", tag="gr", align_bytes=64)
+            xg.append(xgt)
+        for pr in range(2):
+            for g in range(NG):
+                xw = [xs[(pr, g)][:, 0, :].bitcast(F32), xs[(pr, g)][:, 1, :].bitcast(F32)]
+                pt = ptp.tile([P, 2, 256], F32, name="pt", tag="pt")
+                transposes(pt, xw, 0)
+                nc.vector.tensor_copy(out=words_out(xg[g // 2][:, g % 2, :, :], pr), in_=pt[:].rearrange("p u r -> p r u"))
+        for h in range(2):
+            nc.vector.quantize_mx(
+                out=xc[:, 2 * h : 2 * h + 2, :].rearrange("p g n -> p (g n)").bitcast(FP8X4),
+                scales=xsc[:, 2 * h : 2 * h + 2, :].rearrange("p g n -> p (g n)"),
+                in_=xg[h][:].rearrange("p g r t -> p (g r t)"),
+            )
+
+        wf = {}
+        gr = {}
+        wc = {}
+
+        def widen(t, tiles):
+            for a in tiles:
+                w16 = wfp.tile([P, D], BF16, name="wf", tag="wf")
+                nc.scalar.copy(out=w16[:], in_=wbytes[(t, a)][:].bitcast(FP8))
+                wf[(t, a)] = w16
+
+        def prep(t, pr, g):
+            ww = [wf[(t, 2 * pr)][:].bitcast(F32), wf[(t, 2 * pr + 1)][:].bitcast(F32)]
+            if True:
+                if pr == 0 and g % 2 == 0:
+                    grt = grp.tile([P, 2, 512, 4], BF16, name="gr", tag="gr", align_bytes=64)
+                    gr[(t, g // 2)] = grt
+                pt = ptp.tile([P, 2, 256], F32, name="pt", tag="pt")
+                transposes(pt, ww, 256 * g)
+                dst = gr[(t, g // 2)][:, g % 2, 256 * pr : 256 * pr + 256, :]
+                if (pr, g) in G_UNITS:
+                    tmp = tmpp.tile([P, 256, 4], BF16, name="tmp", tag="tmp")
+                    nc.scalar.copy(
+                        out=tmp[:].rearrange("p r t -> p (r t)").bitcast(F32).rearrange("p (r u) -> p r u", u=2),
+                        in_=pt[:].rearrange("p u r -> p r u"),
+                    )
+                    nc.gpsimd.tensor_tensor(
+                        out=dst.rearrange("p r (u e) -> p r u e", u=2),
+                        in0=tmp[:].rearrange("p r (u e) -> p r u e", u=2),
+                        in1=sc[:, g, :, :, :].to_broadcast([P, 256, 2, 2]),
+                        op=MULT,
+                    )
+                else:
+                    nc.vector.tensor_tensor(
+                        out=dst.rearrange("p r (u e) -> p r u e", u=2),
+                        in0=pt[:].bitcast(BF16).rearrange("p u (r e) -> p r u e", e=2),
+                        in1=sc[:, g, :, :, :].to_broadcast([P, 256, 2, 2]),
+                        op=MULT,
+                    )
+
+        def quant(t, h):
+            if h == 0:
+                wct = wcp.tile([P, NG, 512], U32, name="wc", tag="wc", align_bytes=64)
+                wst = wcp.tile([P, NG, 512], U8, name="wsc", tag="wsc", align_bytes=64)
+                wc[t] = (wct, wst)
+            wct, wst = wc[t]
+            nc.vector.quantize_mx(
+                out=wct[:, 2 * h : 2 * h + 2, :].rearrange("p g n -> p (g n)").bitcast(FP8X4),
+                scales=wst[:, 2 * h : 2 * h + 2, :].rearrange("p g n -> p (g n)"),
+                in_=gr[(t, h)][:].rearrange("p g r t -> p (g r t)"),
+            )
+
+        q_flat = out_0.rearrange("s h d -> s (h d)")
+        k_flat = out_1.rearrange("s h d -> s (h d)")
+        v_flat = out_2.rearrange("s h d -> s (h d)")
+
+        accs = {}
+
+        def mm(t, h):
+            wct, wst = wc[t]
+            for m in range(4):
+                if h == 0:
+                    acc = accp.tile([P, 1, 512], F32, name="acc", tag="acc")
+                    accs[(t, m)] = acc
+                for g in (2 * h, 2 * h + 1):
+                    nc.tensor.matmul_mx(
+                        out=accs[(t, m)][:, 0, :],
+                        lhsT=xc[:, g, 128 * m : 128 * m + 128].bitcast(FP8X4),
+                        lhsT_scale=xsc[:, g, 128 * m : 128 * m + 128],
+                        rhs=wct[:, g, :].bitcast(FP8X4),
+                        rhs_scale=wst[:, g, :],
+                        start=(g == 0),
+                        stop=(g == NG - 1),
+                    )
+
+        def finish(t, m):
+            acc = accs[(t, m)]
+            o = op.tile([P, 512], F32, name="o", tag="o")
+            rows = slice(128 * m, 128 * m + 128)
+            if t == 5:
+                if m % 2 == 0:
+                    nc.scalar.copy(out=o[:], in_=acc[:, 0, :])
+                else:
+                    nc.vector.tensor_copy(out=o[:], in_=acc[:, 0, :])
+                nc.sync.dma_start(out=v_flat[rows, :], in_=o[:])
+                return
+            pr = prp.tile([P, 2, 512], F32, name="pr", tag="pr")
+            nc.vector.tensor_tensor(out=pr[:], in0=acc[:].to_broadcast([P, 2, 512]), in1=tab[:, m, :, :], op=MULT)
+            eng = nc.gpsimd if ADD_ON_GPSIMD else nc.vector
+            eng.tensor_tensor(
+                out=o[:].rearrange("p (j q) -> p j q", q=2),
+                in0=pr[:, :, 0:256].rearrange("p q j -> p j q"),
+                in1=pr[:, :, 256:512].rearrange("p q j -> p j q"),
+                op=ADD,
+            )
+            if t < 4:
+                nc.sync.dma_start(out=q_flat[rows, 512 * t : 512 * t + 512], in_=o[:])
+            else:
+                nc.sync.dma_start(out=k_flat[rows, :], in_=o[:])
+
+        widen(0, (0, 1))
+        for t in range(NT):
+            prep(t, 0, 0)
+            prep(t, 0, 1)
+            if t == 0:
+                widen(0, (2, 3))
+            if t + 1 < NT:
+                widen(t + 1, (0, 1, 2, 3))
+            prep(t, 0, 2)
+            if t > 0:
+                finish(t - 1, 0)
+                finish(t - 1, 1)
+            prep(t, 0, 3)
+            if t > 0:
+                finish(t - 1, 2)
+                finish(t - 1, 3)
+            for g in range(NG):
+                prep(t, 1, g)
+            for h in range(2):
+                quant(t, h)
+                mm(t, h)
+        for m in range(4):
+            finish(NT - 1, m)

@@ -14,12 +14,14 @@ FP8 = mybir.dt.float8_e4m3fn
 FP8X4 = mybir.dt.float8_e4m3fn_x4
 MULT = mybir.AluOpType.mult
 ADD = mybir.AluOpType.add
+COPY = mybir.ActivationFunctionType.Copy
 
 P = 128
 NG = 4
 NT = 6
-ADD_ON_GPSIMD = True
-G_UNITS = ((0, 0), (0, 1))
+
+BANKS = ((0, 2), (0, 3), (0, 0), (0, 1), (1, 2), (1, 0), (1, 1), (1, 3))
+LANES = (("B", "B", "V"), ("Y", "Y", "B"), ("Y", "Y", "Y"), ("Y", "Y", "Y"), ("Y", "Y", "Y"), ("Y", "Y", "Y"))
 
 
 def tile_mha_pa_kernel(tc, x, freqs_cos, freqs_sin, wqkv_bytes, wqkv_scale, out_0, out_1, out_2):
@@ -29,9 +31,9 @@ def tile_mha_pa_kernel(tc, x, freqs_cos, freqs_sin, wqkv_bytes, wqkv_scale, out_
         wbp = ctx.enter_context(tc.tile_pool(name="wbp", bufs=24))
         xp = ctx.enter_context(tc.tile_pool(name="xp", bufs=8))
         wfp = ctx.enter_context(tc.tile_pool(name="wfp", bufs=8))
-        grp = ctx.enter_context(tc.tile_pool(name="grp", bufs=2))
+        grp = ctx.enter_context(tc.tile_pool(name="grp", bufs=1))
         tmpp = ctx.enter_context(tc.tile_pool(name="tmpp", bufs=3))
-        wcp = ctx.enter_context(tc.tile_pool(name="wcp", bufs=3))
+        wcp = ctx.enter_context(tc.tile_pool(name="wcp", bufs=2))
         prp = ctx.enter_context(tc.tile_pool(name="prp", bufs=4))
         op = ctx.enter_context(tc.tile_pool(name="op", bufs=4))
         ptp = ctx.enter_context(tc.psum_pool(name="ptp", bufs=4))
@@ -72,14 +74,14 @@ def tile_mha_pa_kernel(tc, x, freqs_cos, freqs_sin, wqkv_bytes, wqkv_scale, out_
             nc.sync.dma_start(out=xt[:], in_=x_pairs[pr, :, :, 512 * g : 512 * g + 512])
             xs[(pr, g)] = xt
 
-        for g in range(NG):
-            load_x(0, g)
         load_w(0, 0)
         load_w(0, 1)
         for g in range(NG):
-            load_x(1, g)
+            load_x(0, g)
         load_w(0, 2)
         load_w(0, 3)
+        for g in range(NG):
+            load_x(1, g)
         for t in range(1, NT):
             for a in range(4):
                 load_w(t, a)
@@ -95,6 +97,8 @@ def tile_mha_pa_kernel(tc, x, freqs_cos, freqs_sin, wqkv_bytes, wqkv_scale, out_
                 op1=ADD,
             )
 
+        ctx.enter_context(tc.manual_schedule())
+
         def transposes(pt, words, w0):
             for u in range(2):
                 for b in range(2):
@@ -104,71 +108,97 @@ def tile_mha_pa_kernel(tc, x, freqs_cos, freqs_sin, wqkv_bytes, wqkv_scale, out_
                         identity=ident[:],
                     )
 
-        def words_out(dst, pr):
-            return (
-                dst
-                .rearrange("p r t -> p (r t)")[:, 1024 * pr : 1024 * pr + 1024]
-                .bitcast(F32)
-                .rearrange("p (r u) -> p r u", u=2)
-            )
-
-        xc = const.tile([P, NG, S], U32, name="xc", tag="xc", align_bytes=64)
-        xsc = const.tile([P, NG, S], U8, name="xsc", tag="xsc", align_bytes=64)
-        xg = []
-        for h in range(2):
-            xgt = grp.tile([P, 2, 512, 4], BF16, name="gr", tag="gr", align_bytes=64)
-            xg.append(xgt)
-        for pr in range(2):
-            for g in range(NG):
-                xw = [xs[(pr, g)][:, 0, :].bitcast(F32), xs[(pr, g)][:, 1, :].bitcast(F32)]
-                pt = ptp.tile([P, 2, 256], F32, name="pt", tag="pt")
-                transposes(pt, xw, 0)
-                nc.vector.tensor_copy(out=words_out(xg[g // 2][:, g % 2, :, :], pr), in_=pt[:].rearrange("p u r -> p r u"))
-        for h in range(2):
-            nc.vector.quantize_mx(
-                out=xc[:, 2 * h : 2 * h + 2, :].rearrange("p g n -> p (g n)").bitcast(FP8X4),
-                scales=xsc[:, 2 * h : 2 * h + 2, :].rearrange("p g n -> p (g n)"),
-                in_=xg[h][:].rearrange("p g r t -> p (g r t)"),
-            )
+        def new_gr(h):
+            return grp.tile([P, 2, 512, 4], BF16, name="gr%d" % h, tag="gr%d" % h, align_bytes=64)
 
         wf = {}
+        pts = {}
+        tmps = {}
         gr = {}
         wc = {}
+        accs = {}
+        prs = {}
 
-        def widen(t, tiles):
-            for a in tiles:
-                w16 = wfp.tile([P, D], BF16, name="wf", tag="wf")
-                nc.scalar.copy(out=w16[:], in_=wbytes[(t, a)][:].bitcast(FP8))
-                wf[(t, a)] = w16
+        def widen(t, a):
+            if t >= NT:
+                return
+            w16 = wfp.tile([P, D], BF16, name="wf", tag="wf")
+            nc.scalar.copy(out=w16[:], in_=wbytes[(t, a)][:].bitcast(FP8))
+            wf[(t, a)] = w16
 
-        def prep(t, pr, g):
+        def lane(t, b):
+            if b in (0, 1, 4):
+                return LANES[t][(0, 1, 4).index(b)]
+            return "V"
+
+        def trans(t, b):
+            if t >= NT:
+                return
+            pr, g = BANKS[b]
             ww = [wf[(t, 2 * pr)][:].bitcast(F32), wf[(t, 2 * pr + 1)][:].bitcast(F32)]
-            if True:
-                if pr == 0 and g % 2 == 0:
-                    grt = grp.tile([P, 2, 512, 4], BF16, name="gr", tag="gr", align_bytes=64)
-                    gr[(t, g // 2)] = grt
-                pt = ptp.tile([P, 2, 256], F32, name="pt", tag="pt")
-                transposes(pt, ww, 256 * g)
-                dst = gr[(t, g // 2)][:, g % 2, 256 * pr : 256 * pr + 256, :]
-                if (pr, g) in G_UNITS:
-                    tmp = tmpp.tile([P, 256, 4], BF16, name="tmp", tag="tmp")
-                    nc.scalar.copy(
-                        out=tmp[:].rearrange("p r t -> p (r t)").bitcast(F32).rearrange("p (r u) -> p r u", u=2),
-                        in_=pt[:].rearrange("p u r -> p r u"),
-                    )
-                    nc.gpsimd.tensor_tensor(
-                        out=dst.rearrange("p r (u e) -> p r u e", u=2),
-                        in0=tmp[:].rearrange("p r (u e) -> p r u e", u=2),
-                        in1=sc[:, g, :, :, :].to_broadcast([P, 256, 2, 2]),
-                        op=MULT,
-                    )
-                else:
-                    nc.vector.tensor_tensor(
-                        out=dst.rearrange("p r (u e) -> p r u e", u=2),
-                        in0=pt[:].bitcast(BF16).rearrange("p u (r e) -> p r u e", e=2),
-                        in1=sc[:, g, :, :, :].to_broadcast([P, 256, 2, 2]),
-                        op=MULT,
-                    )
+            pt = ptp.tile([P, 2, 256], F32, name="pt", tag="pt")
+            transposes(pt, ww, 256 * g)
+            pts[(t, b)] = pt
+
+        def dst_of(t, b):
+            pr, g = BANKS[b]
+            if (t, g // 2) not in gr:
+                gr[(t, g // 2)] = new_gr(g // 2)
+            return gr[(t, g // 2)][:, g % 2, 256 * pr : 256 * pr + 256, :]
+
+        def scale_v(t, b):
+            g = BANKS[b][1]
+            nc.vector.tensor_tensor(
+                out=dst_of(t, b).rearrange("p r (u e) -> p r u e", u=2),
+                in0=pts[(t, b)][:].bitcast(BF16).rearrange("p u (r e) -> p r u e", e=2),
+                in1=sc[:, g, :, :, :].to_broadcast([P, 256, 2, 2]),
+                op=MULT,
+            )
+
+        def evac_s(t, b):
+            if t >= NT or lane(t, b) == "V":
+                return
+            g = BANKS[b][1]
+            pt = pts[(t, b)]
+            if lane(t, b) == "Y":
+                tmp = tmpp.tile([P, 4, 256], BF16, name="tmp", tag="tmp")
+                planes = pt[:].bitcast(BF16).rearrange("p u (r e) -> p u e r", e=2)
+                for u in range(2):
+                    for e in range(2):
+                        nc.scalar.activation(
+                            out=tmp[:, 2 * u + e, :],
+                            in_=planes[:, u, e, :],
+                            func=COPY,
+                            scale=sc[:, g, 0, u, e : e + 1],
+                        )
+            else:
+                tmp = tmpp.tile([P, 256, 4], BF16, name="tmp", tag="tmp")
+                nc.scalar.copy(
+                    out=tmp[:].rearrange("p r t -> p (r t)").bitcast(F32).rearrange("p (r u) -> p r u", u=2),
+                    in_=pt[:].rearrange("p u r -> p r u"),
+                )
+            tmps[(t, b)] = tmp
+
+        def finish_unit(t, b):
+            g = BANKS[b][1]
+            if lane(t, b) == "V":
+                scale_v(t, b)
+            elif lane(t, b) == "Y":
+                nc.gpsimd.tensor_scalar(
+                    out=dst_of(t, b),
+                    in0=tmps[(t, b)][:].rearrange("p t r -> p r t"),
+                    scalar1=1.0,
+                    scalar2=0.0,
+                    op0=MULT,
+                    op1=ADD,
+                )
+            else:
+                nc.gpsimd.tensor_tensor(
+                    out=dst_of(t, b).rearrange("p r (u e) -> p r u e", u=2),
+                    in0=tmps[(t, b)][:].rearrange("p r (u e) -> p r u e", u=2),
+                    in1=sc[:, g, :, :, :].to_broadcast([P, 256, 2, 2]),
+                    op=MULT,
+                )
 
         def quant(t, h):
             if h == 0:
@@ -186,17 +216,15 @@ def tile_mha_pa_kernel(tc, x, freqs_cos, freqs_sin, wqkv_bytes, wqkv_scale, out_
         k_flat = out_1.rearrange("s h d -> s (h d)")
         v_flat = out_2.rearrange("s h d -> s (h d)")
 
-        accs = {}
-
         def mm(t, h):
             wct, wst = wc[t]
             for m in range(4):
                 if h == 0:
-                    acc = accp.tile([P, 1, 512], F32, name="acc", tag="acc")
+                    acc = accp.tile([P, 512, 1], F32, name="acc", tag="acc")
                     accs[(t, m)] = acc
                 for g in (2 * h, 2 * h + 1):
                     nc.tensor.matmul_mx(
-                        out=accs[(t, m)][:, 0, :],
+                        out=accs[(t, m)][:, :, 0],
                         lhsT=xc[:, g, 128 * m : 128 * m + 128].bitcast(FP8X4),
                         lhsT_scale=xsc[:, g, 128 * m : 128 * m + 128],
                         rhs=wct[:, g, :].bitcast(FP8X4),
@@ -205,51 +233,110 @@ def tile_mha_pa_kernel(tc, x, freqs_cos, freqs_sin, wqkv_bytes, wqkv_scale, out_
                         stop=(g == NG - 1),
                     )
 
-        def finish(t, m):
-            acc = accs[(t, m)]
-            o = op.tile([P, 512], F32, name="o", tag="o")
-            rows = slice(128 * m, 128 * m + 128)
-            if t == 5:
-                if m % 2 == 0:
-                    nc.scalar.copy(out=o[:], in_=acc[:, 0, :])
-                else:
-                    nc.vector.tensor_copy(out=o[:], in_=acc[:, 0, :])
-                nc.sync.dma_start(out=v_flat[rows, :], in_=o[:])
+        def rope_v(t, m):
+            if t < 0:
                 return
-            pr = prp.tile([P, 2, 512], F32, name="pr", tag="pr")
-            nc.vector.tensor_tensor(out=pr[:], in0=acc[:].to_broadcast([P, 2, 512]), in1=tab[:, m, :, :], op=MULT)
-            eng = nc.gpsimd if ADD_ON_GPSIMD else nc.vector
-            eng.tensor_tensor(
-                out=o[:].rearrange("p (j q) -> p j q", q=2),
-                in0=pr[:, :, 0:256].rearrange("p q j -> p j q"),
-                in1=pr[:, :, 256:512].rearrange("p q j -> p j q"),
-                op=ADD,
+            pr = prp.tile([P, 512, 2], F32, name="pr", tag="pr")
+            nc.vector.tensor_tensor(
+                out=pr[:],
+                in0=accs[(t, m)][:].to_broadcast([P, 512, 2]),
+                in1=tab[:, m, :, :].rearrange("p q n -> p n q"),
+                op=MULT,
             )
+            prs[(t, m)] = pr
+
+        def add_g(t, m):
+            if t < 0:
+                return
+            o = op.tile([P, 512], F32, name="o", tag="o")
+            pr = prs[(t, m)][:].rearrange("p n q -> p (n q)")
+            nc.gpsimd.tensor_tensor(out=o[:], in0=pr[:, 0:512], in1=pr[:, 512:1024], op=ADD)
+            rows = slice(128 * m, 128 * m + 128)
             if t < 4:
                 nc.sync.dma_start(out=q_flat[rows, 512 * t : 512 * t + 512], in_=o[:])
             else:
                 nc.sync.dma_start(out=k_flat[rows, :], in_=o[:])
 
-        widen(0, (0, 1))
+        def copy_out(m):
+            o = op.tile([P, 512], F32, name="o", tag="o")
+            if m % 2 == 0:
+                nc.scalar.copy(out=o[:], in_=accs[(NT - 1, m)][:, :, 0])
+            else:
+                nc.vector.tensor_copy(out=o[:], in_=accs[(NT - 1, m)][:, :, 0])
+            nc.sync.dma_start(out=v_flat[128 * m : 128 * m + 128, :], in_=o[:])
+
+        xc = const.tile([P, NG, S], U32, name="xc", tag="xc", align_bytes=64)
+        xsc = const.tile([P, NG, S], U8, name="xsc", tag="xsc", align_bytes=64)
+        xg = [new_gr(0), new_gr(1)]
+        def x_unit(pr, g):
+            xw = [xs[(pr, g)][:, 0, :].bitcast(F32), xs[(pr, g)][:, 1, :].bitcast(F32)]
+            pt = ptp.tile([P, 2, 256], F32, name="pt", tag="pt")
+            transposes(pt, xw, 0)
+            nc.vector.tensor_copy(
+                out=xg[g // 2][:, g % 2, :, :]
+                .rearrange("p r t -> p (r t)")[:, 1024 * pr : 1024 * pr + 1024]
+                .bitcast(F32)
+                .rearrange("p (r u) -> p r u", u=2),
+                in_=pt[:].rearrange("p u r -> p r u"),
+            )
+
+        widen(0, 0)
+        widen(0, 1)
+        for g in range(NG):
+            x_unit(0, g)
+        trans(0, 0)
+        evac_s(0, 0)
+        trans(0, 1)
+        evac_s(0, 1)
+        for g in range(NG):
+            x_unit(1, g)
+        trans(0, 2)
+        trans(0, 3)
+        for h in range(2):
+            nc.vector.quantize_mx(
+                out=xc[:, 2 * h : 2 * h + 2, :].rearrange("p g n -> p (g n)").bitcast(FP8X4),
+                scales=xsc[:, 2 * h : 2 * h + 2, :].rearrange("p g n -> p (g n)"),
+                in_=xg[h][:].rearrange("p g r t -> p (g r t)"),
+            )
+
         for t in range(NT):
-            prep(t, 0, 0)
-            prep(t, 0, 1)
-            if t == 0:
-                widen(0, (2, 3))
-            if t + 1 < NT:
-                widen(t + 1, (0, 1, 2, 3))
-            prep(t, 0, 2)
-            if t > 0:
-                finish(t - 1, 0)
-                finish(t - 1, 1)
-            prep(t, 0, 3)
-            if t > 0:
-                finish(t - 1, 2)
-                finish(t - 1, 3)
-            for g in range(NG):
-                prep(t, 1, g)
-            for h in range(2):
-                quant(t, h)
-                mm(t, h)
+            widen(t, 2)
+            widen(t, 3)
+            finish_unit(t, 0)
+            finish_unit(t, 2)
+            finish_unit(t, 1)
+            finish_unit(t, 3)
+            rope_v(t - 1, 0)
+            add_g(t - 1, 0)
+            rope_v(t - 1, 1)
+            add_g(t - 1, 1)
+            trans(t, 4)
+            widen(t + 1, 0)
+            evac_s(t, 4)
+            trans(t, 5)
+            trans(t, 6)
+            trans(t, 7)
+            if lane(t, 4) != "V":
+                finish_unit(t, 4)
+            rope_v(t - 1, 2)
+            add_g(t - 1, 2)
+            rope_v(t - 1, 3)
+            add_g(t - 1, 3)
+            if lane(t, 4) == "V":
+                finish_unit(t, 4)
+            widen(t + 1, 1)
+            trans(t + 1, 0)
+            evac_s(t + 1, 0)
+            finish_unit(t, 5)
+            trans(t + 1, 1)
+            evac_s(t + 1, 1)
+            finish_unit(t, 6)
+            trans(t + 1, 2)
+            finish_unit(t, 7)
+            trans(t + 1, 3)
+            quant(t, 0)
+            mm(t, 0)
+            quant(t, 1)
+            mm(t, 1)
         for m in range(4):
-            finish(NT - 1, m)
+            copy_out(m)

@@ -20,8 +20,8 @@ P = 128
 NG = 4
 NT = 6
 
-BANKS = ((0, 2), (0, 3), (0, 0), (0, 1), (1, 2), (1, 0), (1, 1), (1, 3))
 LANES = (("B", "B", "V"), ("Y", "Y", "B"), ("Y", "Y", "Y"), ("Y", "Y", "Y"), ("Y", "Y", "Y"), ("Y", "Y", "Y"))
+HELPED = ((0, 2), (0, 3), (1, 2))
 
 
 def tile_mha_pa_kernel(tc, x, freqs_cos, freqs_sin, wqkv_bytes, wqkv_scale, out_0, out_1, out_2):
@@ -35,7 +35,7 @@ def tile_mha_pa_kernel(tc, x, freqs_cos, freqs_sin, wqkv_bytes, wqkv_scale, out_
         tmpp = ctx.enter_context(tc.tile_pool(name="tmpp", bufs=3))
         wcp = ctx.enter_context(tc.tile_pool(name="wcp", bufs=2))
         prp = ctx.enter_context(tc.tile_pool(name="prp", bufs=4))
-        op = ctx.enter_context(tc.tile_pool(name="op", bufs=4))
+        op = ctx.enter_context(tc.tile_pool(name="op", bufs=8))
         ptp = ctx.enter_context(tc.psum_pool(name="ptp", bufs=4))
         accp = ctx.enter_context(tc.psum_pool(name="accp", bufs=4))
 
@@ -49,8 +49,6 @@ def tile_mha_pa_kernel(tc, x, freqs_cos, freqs_sin, wqkv_bytes, wqkv_scale, out_
         )
         cosb = const.tile([P, 4, 1, 64], BF16, name="cosb", tag="cosb")
         sinb = const.tile([P, 4, 1, 64], BF16, name="sinb", tag="sinb")
-        nc.sync.dma_start(out=cosb[:, :, 0, :], in_=freqs_cos.rearrange("(m p) i -> p m i", p=P))
-        nc.sync.dma_start(out=sinb[:, :, 0, :], in_=freqs_sin.rearrange("(m p) i -> p m i", p=P))
 
         w_par = wqkv_bytes.rearrange("(j q) k -> q j k", q=2)
 
@@ -74,14 +72,20 @@ def tile_mha_pa_kernel(tc, x, freqs_cos, freqs_sin, wqkv_bytes, wqkv_scale, out_
             nc.sync.dma_start(out=xt[:], in_=x_pairs[pr, :, :, 512 * g : 512 * g + 512])
             xs[(pr, g)] = xt
 
+        nc.sync.dma_start(out=cosb[:, :, 0, :], in_=freqs_cos.rearrange("(m p) i -> p m i", p=P))
+        nc.sync.dma_start(out=sinb[:, :, 0, :], in_=freqs_sin.rearrange("(m p) i -> p m i", p=P))
         load_w(0, 0)
         load_w(0, 1)
-        for g in range(NG):
-            load_x(0, g)
+        load_x(0, 0)
+        load_x(0, 1)
+        load_x(0, 2)
+        load_x(0, 3)
+        load_x(1, 0)
+        load_x(1, 1)
+        load_x(1, 2)
+        load_x(1, 3)
         load_w(0, 2)
         load_w(0, 3)
-        for g in range(NG):
-            load_x(1, g)
         for t in range(1, NT):
             for a in range(4):
                 load_w(t, a)
@@ -111,6 +115,9 @@ def tile_mha_pa_kernel(tc, x, freqs_cos, freqs_sin, wqkv_bytes, wqkv_scale, out_
         def new_gr(h):
             return grp.tile([P, 2, 512, 4], BF16, name="gr%d" % h, tag="gr%d" % h, align_bytes=64)
 
+        def new_bank():
+            return ptp.tile([P, 2, 256], F32, name="pt", tag="pt")
+
         wf = {}
         pts = {}
         tmps = {}
@@ -119,48 +126,42 @@ def tile_mha_pa_kernel(tc, x, freqs_cos, freqs_sin, wqkv_bytes, wqkv_scale, out_
         accs = {}
         prs = {}
 
+        def ok(t):
+            return 0 <= t < NT
+
         def widen(t, a):
-            if t >= NT:
+            if not ok(t):
                 return
             w16 = wfp.tile([P, D], BF16, name="wf", tag="wf")
             nc.scalar.copy(out=w16[:], in_=wbytes[(t, a)][:].bitcast(FP8))
             wf[(t, a)] = w16
 
-        def lane(t, b):
-            if b in (0, 1, 4):
-                return LANES[t][(0, 1, 4).index(b)]
+        def lane(t, unit):
+            if unit in HELPED:
+                return LANES[t][HELPED.index(unit)]
             return "V"
 
-        def trans(t, b):
-            if t >= NT:
+        def trans(t, unit):
+            if not ok(t):
                 return
-            pr, g = BANKS[b]
+            pr, g = unit
             ww = [wf[(t, 2 * pr)][:].bitcast(F32), wf[(t, 2 * pr + 1)][:].bitcast(F32)]
-            pt = ptp.tile([P, 2, 256], F32, name="pt", tag="pt")
+            pt = new_bank()
             transposes(pt, ww, 256 * g)
-            pts[(t, b)] = pt
+            pts[(t, unit)] = pt
 
-        def dst_of(t, b):
-            pr, g = BANKS[b]
+        def dst_of(t, unit):
+            pr, g = unit
             if (t, g // 2) not in gr:
                 gr[(t, g // 2)] = new_gr(g // 2)
             return gr[(t, g // 2)][:, g % 2, 256 * pr : 256 * pr + 256, :]
 
-        def scale_v(t, b):
-            g = BANKS[b][1]
-            nc.vector.tensor_tensor(
-                out=dst_of(t, b).rearrange("p r (u e) -> p r u e", u=2),
-                in0=pts[(t, b)][:].bitcast(BF16).rearrange("p u (r e) -> p r u e", e=2),
-                in1=sc[:, g, :, :, :].to_broadcast([P, 256, 2, 2]),
-                op=MULT,
-            )
-
-        def evac_s(t, b):
-            if t >= NT or lane(t, b) == "V":
+        def evac_s(t, unit):
+            if not ok(t) or lane(t, unit) == "V":
                 return
-            g = BANKS[b][1]
-            pt = pts[(t, b)]
-            if lane(t, b) == "Y":
+            g = unit[1]
+            pt = pts[(t, unit)]
+            if lane(t, unit) == "Y":
                 tmp = tmpp.tile([P, 4, 256], BF16, name="tmp", tag="tmp")
                 planes = pt[:].bitcast(BF16).rearrange("p u (r e) -> p u e r", e=2)
                 for u in range(2):
@@ -177,16 +178,27 @@ def tile_mha_pa_kernel(tc, x, freqs_cos, freqs_sin, wqkv_bytes, wqkv_scale, out_
                     out=tmp[:].rearrange("p r t -> p (r t)").bitcast(F32).rearrange("p (r u) -> p r u", u=2),
                     in_=pt[:].rearrange("p u r -> p r u"),
                 )
-            tmps[(t, b)] = tmp
+            tmps[(t, unit)] = tmp
 
-        def finish_unit(t, b):
-            g = BANKS[b][1]
-            if lane(t, b) == "V":
-                scale_v(t, b)
-            elif lane(t, b) == "Y":
+        def unit_v(t, unit):
+            if not ok(t) or lane(t, unit) != "V":
+                return
+            g = unit[1]
+            nc.vector.tensor_tensor(
+                out=dst_of(t, unit).rearrange("p r (u e) -> p r u e", u=2),
+                in0=pts[(t, unit)][:].bitcast(BF16).rearrange("p u (r e) -> p r u e", e=2),
+                in1=sc[:, g, :, :, :].to_broadcast([P, 256, 2, 2]),
+                op=MULT,
+            )
+
+        def unit_g(t, unit):
+            if not ok(t) or lane(t, unit) == "V":
+                return
+            g = unit[1]
+            if lane(t, unit) == "Y":
                 nc.gpsimd.tensor_scalar(
-                    out=dst_of(t, b),
-                    in0=tmps[(t, b)][:].rearrange("p t r -> p r t"),
+                    out=dst_of(t, unit),
+                    in0=tmps[(t, unit)][:].rearrange("p t r -> p r t"),
                     scalar1=1.0,
                     scalar2=0.0,
                     op0=MULT,
@@ -194,47 +206,50 @@ def tile_mha_pa_kernel(tc, x, freqs_cos, freqs_sin, wqkv_bytes, wqkv_scale, out_
                 )
             else:
                 nc.gpsimd.tensor_tensor(
-                    out=dst_of(t, b).rearrange("p r (u e) -> p r u e", u=2),
-                    in0=tmps[(t, b)][:].rearrange("p r (u e) -> p r u e", u=2),
+                    out=dst_of(t, unit).rearrange("p r (u e) -> p r u e", u=2),
+                    in0=tmps[(t, unit)][:].rearrange("p r (u e) -> p r u e", u=2),
                     in1=sc[:, g, :, :, :].to_broadcast([P, 256, 2, 2]),
                     op=MULT,
                 )
 
-        def quant(t, h):
-            if h == 0:
+        def quant(t, g0, n):
+            if t not in wc:
                 wct = wcp.tile([P, NG, 512], U32, name="wc", tag="wc", align_bytes=64)
                 wst = wcp.tile([P, NG, 512], U8, name="wsc", tag="wsc", align_bytes=64)
                 wc[t] = (wct, wst)
             wct, wst = wc[t]
             nc.vector.quantize_mx(
-                out=wct[:, 2 * h : 2 * h + 2, :].rearrange("p g n -> p (g n)").bitcast(FP8X4),
-                scales=wst[:, 2 * h : 2 * h + 2, :].rearrange("p g n -> p (g n)"),
-                in_=gr[(t, h)][:].rearrange("p g r t -> p (g r t)"),
+                out=wct[:, g0 : g0 + n, :].rearrange("p g n -> p (g n)").bitcast(FP8X4),
+                scales=wst[:, g0 : g0 + n, :].rearrange("p g n -> p (g n)"),
+                in_=gr[(t, g0 // 2)][:, g0 % 2 : g0 % 2 + n, :, :].rearrange("p g r t -> p (g r t)"),
             )
 
         q_flat = out_0.rearrange("s h d -> s (h d)")
         k_flat = out_1.rearrange("s h d -> s (h d)")
         v_flat = out_2.rearrange("s h d -> s (h d)")
 
-        def mm(t, h):
+        def mm(t, passes, first, last, tiles=(0, 1, 2, 3)):
             wct, wst = wc[t]
-            for m in range(4):
-                if h == 0:
+            for m in tiles:
+                if first and t == NT - 1 and m == 3:
+                    acc = ptp.tile([P, 512, 1], F32, name="pt", tag="pt")
+                    accs[(t, m)] = acc
+                elif first:
                     acc = accp.tile([P, 512, 1], F32, name="acc", tag="acc")
                     accs[(t, m)] = acc
-                for g in (2 * h, 2 * h + 1):
+                for g in passes:
                     nc.tensor.matmul_mx(
                         out=accs[(t, m)][:, :, 0],
                         lhsT=xc[:, g, 128 * m : 128 * m + 128].bitcast(FP8X4),
                         lhsT_scale=xsc[:, g, 128 * m : 128 * m + 128],
                         rhs=wct[:, g, :].bitcast(FP8X4),
                         rhs_scale=wst[:, g, :],
-                        start=(g == 0),
-                        stop=(g == NG - 1),
+                        start=(first and g == passes[0]),
+                        stop=(last and g == passes[-1]),
                     )
 
         def rope_v(t, m):
-            if t < 0:
+            if not ok(t):
                 return
             pr = prp.tile([P, 512, 2], F32, name="pr", tag="pr")
             nc.vector.tensor_tensor(
@@ -246,7 +261,7 @@ def tile_mha_pa_kernel(tc, x, freqs_cos, freqs_sin, wqkv_bytes, wqkv_scale, out_
             prs[(t, m)] = pr
 
         def add_g(t, m):
-            if t < 0:
+            if not ok(t):
                 return
             o = op.tile([P, 512], F32, name="o", tag="o")
             pr = prs[(t, m)][:].rearrange("p n q -> p (n q)")
@@ -268,9 +283,10 @@ def tile_mha_pa_kernel(tc, x, freqs_cos, freqs_sin, wqkv_bytes, wqkv_scale, out_
         xc = const.tile([P, NG, S], U32, name="xc", tag="xc", align_bytes=64)
         xsc = const.tile([P, NG, S], U8, name="xsc", tag="xsc", align_bytes=64)
         xg = [new_gr(0), new_gr(1)]
+
         def x_unit(pr, g):
             xw = [xs[(pr, g)][:, 0, :].bitcast(F32), xs[(pr, g)][:, 1, :].bitcast(F32)]
-            pt = ptp.tile([P, 2, 256], F32, name="pt", tag="pt")
+            pt = new_bank()
             transposes(pt, xw, 0)
             nc.vector.tensor_copy(
                 out=xg[g // 2][:, g % 2, :, :]
@@ -280,63 +296,80 @@ def tile_mha_pa_kernel(tc, x, freqs_cos, freqs_sin, wqkv_bytes, wqkv_scale, out_
                 in_=pt[:].rearrange("p u r -> p r u"),
             )
 
-        widen(0, 0)
-        widen(0, 1)
-        for g in range(NG):
-            x_unit(0, g)
-        trans(0, 0)
-        evac_s(0, 0)
-        trans(0, 1)
-        evac_s(0, 1)
-        for g in range(NG):
-            x_unit(1, g)
-        trans(0, 2)
-        trans(0, 3)
-        for h in range(2):
+        def quant_x(h):
             nc.vector.quantize_mx(
                 out=xc[:, 2 * h : 2 * h + 2, :].rearrange("p g n -> p (g n)").bitcast(FP8X4),
                 scales=xsc[:, 2 * h : 2 * h + 2, :].rearrange("p g n -> p (g n)"),
                 in_=xg[h][:].rearrange("p g r t -> p (g r t)"),
             )
 
+        widen(0, 0)
+        widen(0, 1)
+        for g in range(NG):
+            x_unit(0, g)
+        x_unit(1, 0)
+        x_unit(1, 1)
+        trans(0, (0, 2))
+        evac_s(0, (0, 2))
+        trans(0, (0, 3))
+        evac_s(0, (0, 3))
+        x_unit(1, 2)
+        x_unit(1, 3)
+        trans(0, (0, 0))
+        trans(0, (0, 1))
+        quant_x(0)
+        quant_x(1)
+
         for t in range(NT):
-            widen(t, 2)
+            last = t == NT - 1
+            if t == 0:
+                widen(t, 2)
             widen(t, 3)
-            finish_unit(t, 0)
-            finish_unit(t, 2)
-            finish_unit(t, 1)
-            finish_unit(t, 3)
+            unit_g(t, (0, 2))
+            add_g(t - 2, 3)
+            unit_v(t, (0, 0))
+            unit_g(t, (0, 3))
+            unit_v(t, (0, 1))
+            trans(t, (1, 2))
+            widen(t + 1, 0)
+            evac_s(t, (1, 2))
+            trans(t, (1, 0))
+            trans(t, (1, 1))
+            trans(t, (1, 3))
+            widen(t + 1, 1)
+            widen(t + 1, 2)
             rope_v(t - 1, 0)
             add_g(t - 1, 0)
             rope_v(t - 1, 1)
             add_g(t - 1, 1)
-            trans(t, 4)
-            widen(t + 1, 0)
-            evac_s(t, 4)
-            trans(t, 5)
-            trans(t, 6)
-            trans(t, 7)
-            if lane(t, 4) != "V":
-                finish_unit(t, 4)
+            unit_g(t, (1, 2))
+            unit_v(t, (1, 2))
+            unit_v(t, (1, 0))
+            trans(t + 1, (0, 2))
+            evac_s(t + 1, (0, 2))
+            unit_v(t, (1, 1))
+            trans(t + 1, (0, 3))
+            evac_s(t + 1, (0, 3))
             rope_v(t - 1, 2)
+            trans(t + 1, (0, 0))
+            quant(t, 0, 2)
             add_g(t - 1, 2)
-            rope_v(t - 1, 3)
-            add_g(t - 1, 3)
-            if lane(t, 4) == "V":
-                finish_unit(t, 4)
-            widen(t + 1, 1)
-            trans(t + 1, 0)
-            evac_s(t + 1, 0)
-            finish_unit(t, 5)
-            trans(t + 1, 1)
-            evac_s(t + 1, 1)
-            finish_unit(t, 6)
-            trans(t + 1, 2)
-            finish_unit(t, 7)
-            trans(t + 1, 3)
-            quant(t, 0)
-            mm(t, 0)
-            quant(t, 1)
-            mm(t, 1)
+            if last:
+                mm(t, (0, 1), True, False)
+                unit_v(t, (1, 3))
+                quant(t, 2, 1)
+                mm(t, (2,), False, False)
+                rope_v(t - 1, 3)
+                quant(t, 3, 1)
+                mm(t, (3,), False, True)
+            else:
+                mm(t, (0, 1), True, False, (0, 1, 2))
+                unit_v(t, (1, 3))
+                trans(t + 1, (0, 1))
+                rope_v(t - 1, 3)
+                mm(t, (0, 1), True, False, (3,))
+                quant(t, 2, 2)
+                mm(t, (2, 3), False, True)
+        add_g(NT - 2, 3)
         for m in range(4):
             copy_out(m)

@@ -20,7 +20,7 @@ P = 128
 NG = 4
 NT = 6
 
-LANES = (("B", "B", "V"), ("Y", "Y", "B"), ("Y", "Y", "Y"), ("Y", "Y", "Y"), ("Y", "Y", "Y"), ("Y", "Y", "Y"))
+LANES = (("B", "B", "V"), ("Y", "Y", "V"), ("Y", "Y", "V"), ("Y", "Y", "V"), ("Y", "Y", "V"), ("Y", "Y", "V"))
 HELPED = ((0, 2), (0, 3), (1, 2))
 
 

@@ -336,6 +336,8 @@ def tile_mha_pa_kernel(tc, x, freqs_cos, freqs_sin, wqkv_bytes, wqkv_scale, out_
             trans(t, (1, 0))
             trans(t, (1, 1))
             trans(t, (1, 3))
+            if t > 0:
+                mm(t - 1, (2, 3), False, True, (2,))
             widen(t + 1, 1)
             widen(t + 1, 2)
             rope_v(t - 1, 0)
@@ -346,12 +348,16 @@ def tile_mha_pa_kernel(tc, x, freqs_cos, freqs_sin, wqkv_bytes, wqkv_scale, out_
             unit_v(t, (1, 2))
             unit_v(t, (1, 0))
             trans(t + 1, (0, 2))
+            if t > 0:
+                mm(t - 1, (0, 1), True, False, (3,))
             evac_s(t + 1, (0, 2))
             unit_v(t, (1, 1))
             trans(t + 1, (0, 3))
             evac_s(t + 1, (0, 3))
             rope_v(t - 1, 2)
             trans(t + 1, (0, 0))
+            if t > 0:
+                mm(t - 1, (2, 3), False, True, (3,))
             quant(t, 0, 2)
             add_g(t - 1, 2)
             if last:
@@ -363,13 +369,13 @@ def tile_mha_pa_kernel(tc, x, freqs_cos, freqs_sin, wqkv_bytes, wqkv_scale, out_
                 quant(t, 3, 1)
                 mm(t, (3,), False, True)
             else:
-                mm(t, (0, 1), True, False, (0, 1, 2))
+                mm(t, (0, 1), True, False, (0,))
                 unit_v(t, (1, 3))
                 trans(t + 1, (0, 1))
+                mm(t, (0, 1), True, False, (1, 2))
                 rope_v(t - 1, 3)
-                mm(t, (0, 1), True, False, (3,))
                 quant(t, 2, 2)
-                mm(t, (2, 3), False, True)
+                mm(t, (2, 3), False, True, (0, 1))
         add_g(NT - 2, 3)
         for m in range(4):
             copy_out(m)

@@ -20,8 +20,15 @@ P = 128
 NG = 4
 NT = 6
 
-LANES = (("B", "B", "V"), ("Y", "Y", "V"), ("Y", "Y", "V"), ("Y", "Y", "V"), ("Y", "Y", "V"), ("Y", "Y", "V"))
-HELPED = ((0, 2), (0, 3), (1, 2))
+LANES = (
+    ("B", "B", "V", "V"),
+    ("Y", "Y", "V", "V"),
+    ("Y", "Y", "V", "V"),
+    ("Y", "Y", "V", "V"),
+    ("Y", "Y", "V", "V"),
+    ("Y", "Y", "S", "S"),
+)
+HELPED = ((0, 2), (0, 3), (1, 2), (1, 3))
 
 
 def tile_mha_pa_kernel(tc, x, freqs_cos, freqs_sin, wqkv_bytes, wqkv_scale, out_0, out_1, out_2):
@@ -72,10 +79,10 @@ def tile_mha_pa_kernel(tc, x, freqs_cos, freqs_sin, wqkv_bytes, wqkv_scale, out_
             nc.sync.dma_start(out=xt[:], in_=x_pairs[pr, :, :, 512 * g : 512 * g + 512])
             xs[(pr, g)] = xt
 
-        nc.sync.dma_start(out=cosb[:, :, 0, :], in_=freqs_cos.rearrange("(m p) i -> p m i", p=P))
-        nc.sync.dma_start(out=sinb[:, :, 0, :], in_=freqs_sin.rearrange("(m p) i -> p m i", p=P))
         load_w(0, 0)
         load_w(0, 1)
+        nc.sync.dma_start(out=cosb[:, :, 0, :], in_=freqs_cos.rearrange("(m p) i -> p m i", p=P))
+        nc.sync.dma_start(out=sinb[:, :, 0, :], in_=freqs_sin.rearrange("(m p) i -> p m i", p=P))
         load_x(0, 0)
         load_x(0, 1)
         load_x(0, 2)
@@ -161,6 +168,18 @@ def tile_mha_pa_kernel(tc, x, freqs_cos, freqs_sin, wqkv_bytes, wqkv_scale, out_
                 return
             g = unit[1]
             pt = pts[(t, unit)]
+            if lane(t, unit) == "S":
+                planes = pt[:].bitcast(BF16).rearrange("p u (r e) -> p u e r", e=2)
+                dst = dst_of(t, unit)
+                for u in range(2):
+                    for e in range(2):
+                        nc.scalar.activation(
+                            out=dst[:, :, 2 * u + e],
+                            in_=planes[:, u, e, :],
+                            func=COPY,
+                            scale=sc[:, g, 0, u, e : e + 1],
+                        )
+                return
             if lane(t, unit) == "Y":
                 tmp = tmpp.tile([P, 4, 256], BF16, name="tmp", tag="tmp")
                 planes = pt[:].bitcast(BF16).rearrange("p u (r e) -> p u e r", e=2)
@@ -192,7 +211,7 @@ def tile_mha_pa_kernel(tc, x, freqs_cos, freqs_sin, wqkv_bytes, wqkv_scale, out_
             )
 
         def unit_g(t, unit):
-            if not ok(t) or lane(t, unit) == "V":
+            if not ok(t) or lane(t, unit) in ("V", "S"):
                 return
             g = unit[1]
             if lane(t, unit) == "Y":
@@ -231,7 +250,7 @@ def tile_mha_pa_kernel(tc, x, freqs_cos, freqs_sin, wqkv_bytes, wqkv_scale, out_
         def mm(t, passes, first, last, tiles=(0, 1, 2, 3)):
             wct, wst = wc[t]
             for m in tiles:
-                if first and t == NT - 1 and m == 3:
+                if first and t == NT - 1 and m >= 2:
                     acc = ptp.tile([P, 512, 1], F32, name="pt", tag="pt")
                     accs[(t, m)] = acc
                 elif first:
@@ -320,8 +339,7 @@ def tile_mha_pa_kernel(tc, x, freqs_cos, freqs_sin, wqkv_bytes, wqkv_scale, out_
         quant_x(0)
         quant_x(1)
 
-        for t in range(NT):
-            last = t == NT - 1
+        for t in range(NT - 1):
             if t == 0:
                 widen(t, 2)
             widen(t, 3)
@@ -360,22 +378,45 @@ def tile_mha_pa_kernel(tc, x, freqs_cos, freqs_sin, wqkv_bytes, wqkv_scale, out_
                 mm(t - 1, (2, 3), False, True, (3,))
             quant(t, 0, 2)
             add_g(t - 1, 2)
-            if last:
-                mm(t, (0, 1), True, False)
-                unit_v(t, (1, 3))
-                quant(t, 2, 1)
-                mm(t, (2,), False, False)
-                rope_v(t - 1, 3)
-                quant(t, 3, 1)
-                mm(t, (3,), False, True)
-            else:
-                mm(t, (0, 1), True, False, (0,))
-                unit_v(t, (1, 3))
-                trans(t + 1, (0, 1))
-                mm(t, (0, 1), True, False, (1, 2))
-                rope_v(t - 1, 3)
-                quant(t, 2, 2)
-                mm(t, (2, 3), False, True, (0, 1))
-        add_g(NT - 2, 3)
+            mm(t, (0, 1), True, False, (0,))
+            unit_v(t, (1, 3))
+            trans(t + 1, (0, 1))
+            mm(t, (0, 1), True, False, (1, 2))
+            rope_v(t - 1, 3)
+            quant(t, 2, 2)
+            mm(t, (2, 3), False, True, (0, 1))
+
+        t = NT - 1
+        widen(t, 3)
+        unit_g(t, (0, 2))
+        add_g(t - 2, 3)
+        unit_v(t, (0, 0))
+        unit_g(t, (0, 3))
+        unit_v(t, (0, 1))
+        trans(t, (1, 2))
+        evac_s(t, (1, 2))
+        trans(t, (1, 0))
+        trans(t, (1, 1))
+        trans(t, (1, 3))
+        mm(t - 1, (2, 3), False, True, (2,))
+        evac_s(t, (1, 3))
+        rope_v(t - 1, 0)
+        add_g(t - 1, 0)
+        unit_v(t, (1, 0))
+        mm(t - 1, (0, 1), True, False, (3,))
+        mm(t - 1, (2, 3), False, True, (3,))
+        unit_v(t, (1, 1))
+        rope_v(t - 1, 1)
+        quant(t, 0, 2)
+        mm(t, (0, 1), True, False)
+        quant(t, 2, 1)
+        add_g(t - 1, 1)
+        mm(t, (2,), False, False)
+        rope_v(t - 1, 2)
+        add_g(t - 1, 2)
+        rope_v(t - 1, 3)
+        add_g(t - 1, 3)
+        quant(t, 3, 1)
+        mm(t, (3,), False, True)
         for m in range(4):
             copy_out(m)

@@ -22,10 +22,10 @@ NT = 6
 
 LANES = (
     ("B", "B", "V", "V"),
-    ("Y", "Y", "V", "V"),
-    ("Y", "Y", "V", "V"),
-    ("Y", "Y", "V", "V"),
-    ("Y", "Y", "V", "V"),
+    ("Y", "Y", "H", "V"),
+    ("Y", "Y", "H", "V"),
+    ("Y", "Y", "H", "V"),
+    ("Y", "Y", "H", "V"),
     ("Y", "Y", "S", "S"),
 )
 HELPED = ((0, 2), (0, 3), (1, 2), (1, 3))
@@ -180,14 +180,15 @@ def tile_mha_pa_kernel(tc, x, freqs_cos, freqs_sin, wqkv_bytes, wqkv_scale, out_
                             scale=sc[:, g, 0, u, e : e + 1],
                         )
                 return
-            if lane(t, unit) == "Y":
+            if lane(t, unit) in ("Y", "H"):
+                r0 = 128 if lane(t, unit) == "H" else 0
                 tmp = tmpp.tile([P, 4, 256], BF16, name="tmp", tag="tmp")
                 planes = pt[:].bitcast(BF16).rearrange("p u (r e) -> p u e r", e=2)
                 for u in range(2):
                     for e in range(2):
                         nc.scalar.activation(
-                            out=tmp[:, 2 * u + e, :],
-                            in_=planes[:, u, e, :],
+                            out=tmp[:, 2 * u + e, r0:256],
+                            in_=planes[:, u, e, r0:256],
                             func=COPY,
                             scale=sc[:, g, 0, u, e : e + 1],
                         )
@@ -200,13 +201,14 @@ def tile_mha_pa_kernel(tc, x, freqs_cos, freqs_sin, wqkv_bytes, wqkv_scale, out_
             tmps[(t, unit)] = tmp
 
         def unit_v(t, unit):
-            if not ok(t) or lane(t, unit) != "V":
+            if not ok(t) or lane(t, unit) not in ("V", "H"):
                 return
             g = unit[1]
+            rows = 128 if lane(t, unit) == "H" else 256
             nc.vector.tensor_tensor(
-                out=dst_of(t, unit).rearrange("p r (u e) -> p r u e", u=2),
-                in0=pts[(t, unit)][:].bitcast(BF16).rearrange("p u (r e) -> p r u e", e=2),
-                in1=sc[:, g, :, :, :].to_broadcast([P, 256, 2, 2]),
+                out=dst_of(t, unit)[:, 0:rows, :].rearrange("p r (u e) -> p r u e", u=2),
+                in0=pts[(t, unit)][:].bitcast(BF16).rearrange("p u (r e) -> p r u e", e=2)[:, 0:rows, :, :],
+                in1=sc[:, g, :, :, :].to_broadcast([P, rows, 2, 2]),
                 op=MULT,
             )
 
@@ -214,10 +216,11 @@ def tile_mha_pa_kernel(tc, x, freqs_cos, freqs_sin, wqkv_bytes, wqkv_scale, out_
             if not ok(t) or lane(t, unit) in ("V", "S"):
                 return
             g = unit[1]
-            if lane(t, unit) == "Y":
+            if lane(t, unit) in ("Y", "H"):
+                r0 = 128 if lane(t, unit) == "H" else 0
                 nc.gpsimd.tensor_scalar(
-                    out=dst_of(t, unit),
-                    in0=tmps[(t, unit)][:].rearrange("p t r -> p r t"),
+                    out=dst_of(t, unit)[:, r0:256, :],
+                    in0=tmps[(t, unit)][:, :, r0:256].rearrange("p t r -> p r t"),
                     scalar1=1.0,
                     scalar2=0.0,
                     op0=MULT,

@@ -54,8 +54,8 @@ def tile_mha_pa_kernel(tc, x, freqs_cos, freqs_sin, wqkv_bytes, wqkv_scale, out_
             out=sc[:, :, 0, :, :],
             in_=wqkv_scale.rearrange("o (g p u e) -> p (o g) u e", p=P, u=2, e=2),
         )
-        cosb = const.tile([P, 4, 1, 64], BF16, name="cosb", tag="cosb")
-        sinb = const.tile([P, 4, 1, 64], BF16, name="sinb", tag="sinb")
+        cosb = const.tile([P, 4, 64], BF16, name="cosb", tag="cosb")
+        sinb = const.tile([P, 4, 64], BF16, name="sinb", tag="sinb")
 
         w_par = wqkv_bytes.rearrange("(j q) k -> q j k", q=2)
 
@@ -79,34 +79,24 @@ def tile_mha_pa_kernel(tc, x, freqs_cos, freqs_sin, wqkv_bytes, wqkv_scale, out_
             nc.sync.dma_start(out=xt[:], in_=x_pairs[pr, :, :, 512 * g : 512 * g + 512])
             xs[(pr, g)] = xt
 
-        load_w(0, 0)
-        load_w(0, 1)
-        nc.sync.dma_start(out=cosb[:, :, 0, :], in_=freqs_cos.rearrange("(m p) i -> p m i", p=P))
-        nc.sync.dma_start(out=sinb[:, :, 0, :], in_=freqs_sin.rearrange("(m p) i -> p m i", p=P))
-        load_x(0, 0)
-        load_x(0, 1)
-        load_x(0, 2)
-        load_x(0, 3)
-        load_x(1, 0)
-        load_x(1, 1)
-        load_x(1, 2)
-        load_x(1, 3)
-        load_w(0, 2)
-        load_w(0, 3)
+        for a in range(4):
+            load_w(0, a)
+        load_w(1, 0)
+        nc.sync.dma_start(out=cosb[:], in_=freqs_cos.rearrange("(m p) i -> p m i", p=P))
+        nc.sync.dma_start(out=sinb[:], in_=freqs_sin.rearrange("(m p) i -> p m i", p=P))
+        for pr in range(2):
+            for g in range(NG):
+                load_x(pr, g)
         for t in range(1, NT):
             for a in range(4):
-                load_w(t, a)
+                if (t, a) != (1, 0):
+                    load_w(t, a)
 
-        tab = const.tile([P, 4, 2, 512], F32, name="tab", tag="tab")
-        for q, f, src, sign in ((0, 0, cosb, 1.0), (0, 1, sinb, -1.0), (1, 0, sinb, 1.0), (1, 1, cosb, 1.0)):
-            nc.gpsimd.tensor_scalar(
-                out=tab[:, :, q, 256 * f : 256 * f + 256].rearrange("p m (h i) -> p m h i", h=4),
-                in0=src[:].to_broadcast([P, 4, 4, 64]),
-                scalar1=sign,
-                scalar2=0.0,
-                op0=MULT,
-                op1=ADD,
-            )
+        tab = const.tile([P, 4, 2, 1, 64, 2], BF16, name="tab", tag="tab")
+
+        def tables():
+            for q, f, src, sign in ((0, 0, cosb, 1.0), (0, 1, sinb, -1.0), (1, 0, sinb, 1.0), (1, 1, cosb, 1.0)):
+                nc.gpsimd.tensor_scalar(out=tab[:, :, f, 0, :, q], in0=src[:], scalar1=sign, scalar2=0.0, op0=MULT, op1=ADD)
 
         ctx.enter_context(tc.manual_schedule())
 
@@ -136,11 +126,14 @@ def tile_mha_pa_kernel(tc, x, freqs_cos, freqs_sin, wqkv_bytes, wqkv_scale, out_
         def ok(t):
             return 0 <= t < NT
 
-        def widen(t, a):
+        def widen(t, a, by_vector=False):
             if not ok(t):
                 return
             w16 = wfp.tile([P, D], BF16, name="wf", tag="wf")
-            nc.scalar.copy(out=w16[:], in_=wbytes[(t, a)][:].bitcast(FP8))
+            if by_vector:
+                nc.vector.tensor_copy(out=w16[:], in_=wbytes[(t, a)][:].bitcast(FP8))
+            else:
+                nc.scalar.copy(out=w16[:], in_=wbytes[(t, a)][:].bitcast(FP8))
             wf[(t, a)] = w16
 
         def lane(t, unit):
@@ -275,9 +268,9 @@ def tile_mha_pa_kernel(tc, x, freqs_cos, freqs_sin, wqkv_bytes, wqkv_scale, out_
                 return
             pr = prp.tile([P, 512, 2], F32, name="pr", tag="pr")
             nc.vector.tensor_tensor(
-                out=pr[:],
-                in0=accs[(t, m)][:].to_broadcast([P, 512, 2]),
-                in1=tab[:, m, :, :].rearrange("p q n -> p n q"),
+                out=pr[:].rearrange("p (f h i) q -> p f h i q", f=2, h=4),
+                in0=accs[(t, m)][:].rearrange("p (f h i) o -> p f h i o", f=2, h=4).to_broadcast([P, 2, 4, 64, 2]),
+                in1=tab[:, m, :, :, :, :].to_broadcast([P, 2, 4, 64, 2]),
                 op=MULT,
             )
             prs[(t, m)] = pr
@@ -304,13 +297,17 @@ def tile_mha_pa_kernel(tc, x, freqs_cos, freqs_sin, wqkv_bytes, wqkv_scale, out_
 
         xc = const.tile([P, NG, S], U32, name="xc", tag="xc", align_bytes=64)
         xsc = const.tile([P, NG, S], U8, name="xsc", tag="xsc", align_bytes=64)
-        xg = [new_gr(0), new_gr(1)]
+        xg = [
+            const.tile([P, 2, 512, 4], BF16, name="xg0", tag="xg0", align_bytes=64),
+            const.tile([P, 2, 512, 4], BF16, name="xg1", tag="xg1", align_bytes=64),
+        ]
 
         def x_unit(pr, g):
             xw = [xs[(pr, g)][:, 0, :].bitcast(F32), xs[(pr, g)][:, 1, :].bitcast(F32)]
-            pt = new_bank()
+            pt = accp.tile([P, 2, 256], F32, name="acc", tag="acc")
             transposes(pt, xw, 0)
-            nc.vector.tensor_copy(
+            copy = nc.vector.tensor_copy if pr == 0 else nc.scalar.copy
+            copy(
                 out=xg[g // 2][:, g % 2, :, :]
                 .rearrange("p r t -> p (r t)")[:, 1024 * pr : 1024 * pr + 1024]
                 .bitcast(F32)
@@ -325,26 +322,51 @@ def tile_mha_pa_kernel(tc, x, freqs_cos, freqs_sin, wqkv_bytes, wqkv_scale, out_
                 in_=xg[h][:].rearrange("p g r t -> p (g r t)"),
             )
 
-        widen(0, 0)
+        widen(0, 0, by_vector=True)
         widen(0, 1)
-        for g in range(NG):
-            x_unit(0, g)
-        x_unit(1, 0)
-        x_unit(1, 1)
-        trans(0, (0, 2))
-        evac_s(0, (0, 2))
-        trans(0, (0, 3))
-        evac_s(0, (0, 3))
-        x_unit(1, 2)
-        x_unit(1, 3)
+        widen(0, 2, by_vector=True)
+        widen(0, 3, by_vector=True)
+        widen(1, 0)
+        tables()
         trans(0, (0, 0))
         trans(0, (0, 1))
+        trans(0, (0, 2))
+        trans(0, (0, 3))
+        unit_v(0, (0, 0))
+        unit_v(0, (0, 1))
+        evac_s(0, (0, 2))
+        evac_s(0, (0, 3))
+        for g in range(NG):
+            x_unit(0, g)
+        trans(0, (1, 0))
+        trans(0, (1, 1))
+        for g in range(NG):
+            x_unit(1, g)
+        unit_g(0, (0, 2))
+        unit_v(0, (1, 0))
+        unit_g(0, (0, 3))
+        unit_v(0, (1, 1))
+        trans(0, (1, 2))
+        trans(0, (1, 3))
+        widen(1, 1)
+        unit_v(0, (1, 2))
+        unit_v(0, (1, 3))
+        trans(1, (0, 2))
+        evac_s(1, (0, 2))
+        trans(1, (0, 3))
+        evac_s(1, (0, 3))
+        trans(1, (0, 0))
+        widen(1, 2)
         quant_x(0)
         quant_x(1)
+        quant(0, 0, 2)
+        mm(0, (0, 1), True, False, (0,))
+        trans(1, (0, 1))
+        mm(0, (0, 1), True, False, (1, 2))
+        quant(0, 2, 2)
+        mm(0, (2, 3), False, True, (0, 1))
 
-        for t in range(NT - 1):
-            if t == 0:
-                widen(t, 2)
+        for t in range(1, NT - 1):
             widen(t, 3)
             unit_g(t, (0, 2))
             add_g(t - 2, 3)

@@ -26,8 +26,9 @@ LANES = (
     ("Y", "Y", "H", "V"),
     ("Y", "Y", "H", "V"),
     ("Y", "Y", "H", "V"),
-    ("Y", "Y", "S", "S"),
+    ("Y", "Y", "T", "T"),
 )
+MORE_LANES = {(5, 1, 0): "T", (5, 1, 1): "T"}
 HELPED = ((0, 2), (0, 3), (1, 2), (1, 3))
 
 
@@ -40,6 +41,7 @@ def tile_mha_pa_kernel(tc, x, freqs_cos, freqs_sin, wqkv_bytes, wqkv_scale, out_
         wfp = ctx.enter_context(tc.tile_pool(name="wfp", bufs=8))
         grp = ctx.enter_context(tc.tile_pool(name="grp", bufs=1))
         tmpp = ctx.enter_context(tc.tile_pool(name="tmpp", bufs=3))
+        tmqp = ctx.enter_context(tc.tile_pool(name="tmqp", bufs=2))
         wcp = ctx.enter_context(tc.tile_pool(name="wcp", bufs=2))
         prp = ctx.enter_context(tc.tile_pool(name="prp", bufs=4))
         op = ctx.enter_context(tc.tile_pool(name="op", bufs=8))
@@ -139,7 +141,7 @@ def tile_mha_pa_kernel(tc, x, freqs_cos, freqs_sin, wqkv_bytes, wqkv_scale, out_
         def lane(t, unit):
             if unit in HELPED:
                 return LANES[t][HELPED.index(unit)]
-            return "V"
+            return MORE_LANES.get((t, unit[0], unit[1]), "V")
 
         def trans(t, unit):
             if not ok(t):
@@ -173,9 +175,12 @@ def tile_mha_pa_kernel(tc, x, freqs_cos, freqs_sin, wqkv_bytes, wqkv_scale, out_
                             scale=sc[:, g, 0, u, e : e + 1],
                         )
                 return
-            if lane(t, unit) in ("Y", "H"):
+            if lane(t, unit) in ("Y", "H", "T"):
                 r0 = 128 if lane(t, unit) == "H" else 0
-                tmp = tmpp.tile([P, 4, 256], BF16, name="tmp", tag="tmp")
+                if lane(t, unit) == "T":
+                    tmp = tmqp.tile([P, 4, 256], BF16, name="tmq", tag="tmq")
+                else:
+                    tmp = tmpp.tile([P, 4, 256], BF16, name="tmp", tag="tmp")
                 planes = pt[:].bitcast(BF16).rearrange("p u (r e) -> p u e r", e=2)
                 for u in range(2):
                     for e in range(2):
@@ -185,6 +190,9 @@ def tile_mha_pa_kernel(tc, x, freqs_cos, freqs_sin, wqkv_bytes, wqkv_scale, out_
                             func=COPY,
                             scale=sc[:, g, 0, u, e : e + 1],
                         )
+                if lane(t, unit) == "T":
+                    nc.scalar.copy(out=dst_of(t, unit), in_=tmp[:].rearrange("p t r -> p r t"))
+                    return
             else:
                 tmp = tmpp.tile([P, 256, 4], BF16, name="tmp", tag="tmp")
                 nc.scalar.copy(
@@ -206,7 +214,7 @@ def tile_mha_pa_kernel(tc, x, freqs_cos, freqs_sin, wqkv_bytes, wqkv_scale, out_
             )
 
         def unit_g(t, unit):
-            if not ok(t) or lane(t, unit) in ("V", "S"):
+            if not ok(t) or lane(t, unit) in ("V", "S", "T"):
                 return
             g = unit[1]
             if lane(t, unit) in ("Y", "H"):
@@ -406,39 +414,40 @@ def tile_mha_pa_kernel(tc, x, freqs_cos, freqs_sin, wqkv_bytes, wqkv_scale, out_
             mm(t, (0, 1), True, False, (0,))
             unit_v(t, (1, 3))
             trans(t + 1, (0, 1))
+            if t == NT - 2:
+                widen(t + 1, 3)
+                trans(t + 1, (1, 0))
+                evac_s(t + 1, (1, 0))
+                trans(t + 1, (1, 1))
+                evac_s(t + 1, (1, 1))
             mm(t, (0, 1), True, False, (1, 2))
             rope_v(t - 1, 3)
             quant(t, 2, 2)
             mm(t, (2, 3), False, True, (0, 1))
 
         t = NT - 1
-        widen(t, 3)
         unit_g(t, (0, 2))
         add_g(t - 2, 3)
         unit_v(t, (0, 0))
         unit_g(t, (0, 3))
         unit_v(t, (0, 1))
+        mm(t - 1, (2, 3), False, True, (2,))
         trans(t, (1, 2))
         evac_s(t, (1, 2))
-        trans(t, (1, 0))
-        trans(t, (1, 1))
+        mm(t - 1, (0, 1), True, False, (3,))
         trans(t, (1, 3))
-        mm(t - 1, (2, 3), False, True, (2,))
         evac_s(t, (1, 3))
+        mm(t - 1, (2, 3), False, True, (3,))
         rope_v(t - 1, 0)
         add_g(t - 1, 0)
-        unit_v(t, (1, 0))
-        mm(t - 1, (0, 1), True, False, (3,))
-        mm(t - 1, (2, 3), False, True, (3,))
-        unit_v(t, (1, 1))
         rope_v(t - 1, 1)
+        add_g(t - 1, 1)
         quant(t, 0, 2)
         mm(t, (0, 1), True, False)
-        quant(t, 2, 1)
-        add_g(t - 1, 1)
-        mm(t, (2,), False, False)
         rope_v(t - 1, 2)
         add_g(t - 1, 2)
+        quant(t, 2, 1)
+        mm(t, (2,), False, False)
         rope_v(t - 1, 3)
         add_g(t - 1, 3)
         quant(t, 3, 1)

@@ -399,28 +399,25 @@ def tile_mha_pa_kernel(tc, x, freqs_cos, freqs_sin, wqkv_bytes, wqkv_scale, out_
             unit_v(t, (1, 2))
             unit_v(t, (1, 0))
             trans(t + 1, (0, 2))
-            if t > 0:
-                mm(t - 1, (0, 1), True, False, (3,))
+            mm(t - 1, (0, 1), True, False, (3,))
             evac_s(t + 1, (0, 2))
-            unit_v(t, (1, 1))
+            rope_v(t - 1, 2)
+            add_g(t - 1, 2)
             trans(t + 1, (0, 3))
             evac_s(t + 1, (0, 3))
-            rope_v(t - 1, 2)
+            unit_v(t, (1, 1))
             trans(t + 1, (0, 0))
-            if t > 0:
-                mm(t - 1, (2, 3), False, True, (3,))
-            quant(t, 0, 2)
-            add_g(t - 1, 2)
-            mm(t, (0, 1), True, False, (0,))
+            mm(t - 1, (2, 3), False, True, (3,))
             unit_v(t, (1, 3))
             trans(t + 1, (0, 1))
+            quant(t, 0, 2)
             if t == NT - 2:
                 widen(t + 1, 3)
                 trans(t + 1, (1, 0))
                 evac_s(t + 1, (1, 0))
                 trans(t + 1, (1, 1))
                 evac_s(t + 1, (1, 1))
-            mm(t, (0, 1), True, False, (1, 2))
+            mm(t, (0, 1), True, False, (0, 1, 2))
             rope_v(t - 1, 3)
             quant(t, 2, 2)
             mm(t, (2, 3), False, True, (0, 1))

@@ -21,7 +21,7 @@ NG = 4
 NT = 6
 
 LANES = (
-    ("B", "B", "V", "V"),
+    ("Y", "Y", "V", "V"),
     ("Y", "Y", "H", "V"),
     ("Y", "Y", "H", "V"),
     ("Y", "Y", "H", "V"),
@@ -84,6 +84,7 @@ def tile_mha_pa_kernel(tc, x, freqs_cos, freqs_sin, wqkv_bytes, wqkv_scale, out_
         for a in range(4):
             load_w(0, a)
         load_w(1, 0)
+        load_w(1, 1)
         nc.sync.dma_start(out=cosb[:], in_=freqs_cos.rearrange("(m p) i -> p m i", p=P))
         nc.sync.dma_start(out=sinb[:], in_=freqs_sin.rearrange("(m p) i -> p m i", p=P))
         for pr in range(2):
@@ -91,7 +92,7 @@ def tile_mha_pa_kernel(tc, x, freqs_cos, freqs_sin, wqkv_bytes, wqkv_scale, out_
                 load_x(pr, g)
         for t in range(1, NT):
             for a in range(4):
-                if (t, a) != (1, 0):
+                if (t, a) not in ((1, 0), (1, 1)):
                     load_w(t, a)
 
         tab = const.tile([P, 4, 2, 1, 64, 2], BF16, name="tab", tag="tab")
@@ -314,8 +315,7 @@ def tile_mha_pa_kernel(tc, x, freqs_cos, freqs_sin, wqkv_bytes, wqkv_scale, out_
             xw = [xs[(pr, g)][:, 0, :].bitcast(F32), xs[(pr, g)][:, 1, :].bitcast(F32)]
             pt = accp.tile([P, 2, 256], F32, name="acc", tag="acc")
             transposes(pt, xw, 0)
-            copy = nc.vector.tensor_copy if pr == 0 else nc.scalar.copy
-            copy(
+            nc.scalar.copy(
                 out=xg[g // 2][:, g % 2, :, :]
                 .rearrange("p r t -> p (r t)")[:, 1024 * pr : 1024 * pr + 1024]
                 .bitcast(F32)
@@ -334,7 +334,8 @@ def tile_mha_pa_kernel(tc, x, freqs_cos, freqs_sin, wqkv_bytes, wqkv_scale, out_
         widen(0, 1)
         widen(0, 2, by_vector=True)
         widen(0, 3, by_vector=True)
-        widen(1, 0)
+        widen(1, 0, by_vector=True)
+        widen(1, 1)
         tables()
         trans(0, (0, 0))
         trans(0, (0, 1))
@@ -344,19 +345,20 @@ def tile_mha_pa_kernel(tc, x, freqs_cos, freqs_sin, wqkv_bytes, wqkv_scale, out_
         unit_v(0, (0, 1))
         evac_s(0, (0, 2))
         evac_s(0, (0, 3))
-        for g in range(NG):
-            x_unit(0, g)
         trans(0, (1, 0))
+        x_unit(0, 0)
         trans(0, (1, 1))
-        for g in range(NG):
-            x_unit(1, g)
+        x_unit(0, 1)
         unit_g(0, (0, 2))
         unit_v(0, (1, 0))
+        trans(0, (1, 2))
+        x_unit(0, 2)
         unit_g(0, (0, 3))
         unit_v(0, (1, 1))
-        trans(0, (1, 2))
         trans(0, (1, 3))
-        widen(1, 1)
+        x_unit(0, 3)
+        for g in range(NG):
+            x_unit(1, g)
         unit_v(0, (1, 2))
         unit_v(0, (1, 3))
         trans(1, (0, 2))
@@ -365,13 +367,13 @@ def tile_mha_pa_kernel(tc, x, freqs_cos, freqs_sin, wqkv_bytes, wqkv_scale, out_
         evac_s(1, (0, 3))
         trans(1, (0, 0))
         widen(1, 2)
-        quant_x(0)
-        quant_x(1)
         quant(0, 0, 2)
+        quant_x(0)
         mm(0, (0, 1), True, False, (0,))
         trans(1, (0, 1))
         mm(0, (0, 1), True, False, (1, 2))
         quant(0, 2, 2)
+        quant_x(1)
         mm(0, (2, 3), False, True, (0, 1))
 
         for t in range(1, NT - 1):

@@ -37,7 +37,7 @@ def tile_mha_pa_kernel(tc, x, freqs_cos, freqs_sin, wqkv_bytes, wqkv_scale, out_
     with ExitStack() as ctx:
         const = ctx.enter_context(tc.tile_pool(name="const", bufs=1))
         wbp = ctx.enter_context(tc.tile_pool(name="wbp", bufs=24))
-        xp = ctx.enter_context(tc.tile_pool(name="xp", bufs=8))
+        xp = ctx.enter_context(tc.tile_pool(name="xp", bufs=4))
         wfp = ctx.enter_context(tc.tile_pool(name="wfp", bufs=8))
         grp = ctx.enter_context(tc.tile_pool(name="grp", bufs=1))
         tmpp = ctx.enter_context(tc.tile_pool(name="tmpp", bufs=3))
@@ -74,12 +74,11 @@ def tile_mha_pa_kernel(tc, x, freqs_cos, freqs_sin, wqkv_bytes, wqkv_scale, out_
             wbytes[(t, a)] = wb
 
         xs = {}
-        x_pairs = x.rearrange("(r m p) k -> r p m k", m=2, p=P)
 
-        def load_x(pr, g):
-            xt = xp.tile([P, 2, 512], BF16, name="xs", tag="xs")
-            nc.sync.dma_start(out=xt[:], in_=x_pairs[pr, :, :, 512 * g : 512 * g + 512])
-            xs[(pr, g)] = xt
+        def load_x(m):
+            xt = xp.tile([P, D], BF16, name="xs", tag="xs")
+            nc.sync.dma_start(out=xt[:], in_=x[128 * m : 128 * m + 128, :])
+            xs[m] = xt
 
         for a in range(4):
             load_w(0, a)
@@ -87,9 +86,8 @@ def tile_mha_pa_kernel(tc, x, freqs_cos, freqs_sin, wqkv_bytes, wqkv_scale, out_
         load_w(1, 1)
         nc.sync.dma_start(out=cosb[:], in_=freqs_cos.rearrange("(m p) i -> p m i", p=P))
         nc.sync.dma_start(out=sinb[:], in_=freqs_sin.rearrange("(m p) i -> p m i", p=P))
-        for pr in range(2):
-            for g in range(NG):
-                load_x(pr, g)
+        for m in range(4):
+            load_x(m)
         for t in range(1, NT):
             for a in range(4):
                 if (t, a) not in ((1, 0), (1, 1)):
@@ -300,9 +298,10 @@ def tile_mha_pa_kernel(tc, x, freqs_cos, freqs_sin, wqkv_bytes, wqkv_scale, out_
             o = op.tile([P, 512], F32, name="o", tag="o")
             if m % 2 == 0:
                 nc.scalar.copy(out=o[:], in_=accs[(NT - 1, m)][:, :, 0])
+                nc.scalar.dma_start(out=v_flat[128 * m : 128 * m + 128, :], in_=o[:])
             else:
                 nc.vector.tensor_copy(out=o[:], in_=accs[(NT - 1, m)][:, :, 0])
-            nc.sync.dma_start(out=v_flat[128 * m : 128 * m + 128, :], in_=o[:])
+                nc.sync.dma_start(out=v_flat[128 * m : 128 * m + 128, :], in_=o[:])
 
         xc = const.tile([P, NG, S], U32, name="xc", tag="xc", align_bytes=64)
         xsc = const.tile([P, NG, S], U8, name="xsc", tag="xsc", align_bytes=64)
@@ -312,9 +311,9 @@ def tile_mha_pa_kernel(tc, x, freqs_cos, freqs_sin, wqkv_bytes, wqkv_scale, out_
         ]
 
         def x_unit(pr, g):
-            xw = [xs[(pr, g)][:, 0, :].bitcast(F32), xs[(pr, g)][:, 1, :].bitcast(F32)]
+            xw = [xs[2 * pr][:].bitcast(F32), xs[2 * pr + 1][:].bitcast(F32)]
             pt = accp.tile([P, 2, 256], F32, name="acc", tag="acc")
-            transposes(pt, xw, 0)
+            transposes(pt, xw, 256 * g)
             nc.scalar.copy(
                 out=xg[g // 2][:, g % 2, :, :]
                 .rearrange("p r t -> p (r t)")[:, 1024 * pr : 1024 * pr + 1024]

from contextlib import ExitStack

import concourse.mybir as mybir
from concourse.masks import make_identity

S, D = 512, 2048
FLOPS = 2 * 512 * 3072 * 2048

F32 = mybir.dt.float32
BF16 = mybir.dt.bfloat16
U32 = mybir.dt.uint32
U8 = mybir.dt.uint8
FP8 = mybir.dt.float8_e4m3fn
FP8X4 = mybir.dt.float8_e4m3fn_x4
MULT = mybir.AluOpType.mult
ADD = mybir.AluOpType.add
COPY = mybir.ActivationFunctionType.Copy

P = 128
NG = 4
NT = 6

LANES = (
    ("Y", "Y", "V", "V"),
    ("Y", "Y", "H", "V"),
    ("Y", "Y", "H", "V"),
    ("Y", "Y", "H", "V"),
    ("Y", "Y", "H", "V"),
    ("Y", "Y", "T", "T"),
)
MORE_LANES = {(5, 1, 0): "T", (5, 1, 1): "T"}
HELPED = ((0, 2), (0, 3), (1, 2), (1, 3))


def tile_mha_pa_kernel(tc, x, freqs_cos, freqs_sin, wqkv_bytes, wqkv_scale, out_0, out_1, out_2):
    nc = tc.nc
    with ExitStack() as ctx:
        const = ctx.enter_context(tc.tile_pool(name="const", bufs=1))
        wbp = ctx.enter_context(tc.tile_pool(name="wbp", bufs=24))
        xp = ctx.enter_context(tc.tile_pool(name="xp", bufs=4))
        wfp = ctx.enter_context(tc.tile_pool(name="wfp", bufs=8))
        grp = ctx.enter_context(tc.tile_pool(name="grp", bufs=1))
        tmpp = ctx.enter_context(tc.tile_pool(name="tmpp", bufs=3))
        tmqp = ctx.enter_context(tc.tile_pool(name="tmqp", bufs=2))
        wcp = ctx.enter_context(tc.tile_pool(name="wcp", bufs=2))
        prp = ctx.enter_context(tc.tile_pool(name="prp", bufs=4))
        op = ctx.enter_context(tc.tile_pool(name="op", bufs=8))
        ptp = ctx.enter_context(tc.psum_pool(name="ptp", bufs=4))
        accp = ctx.enter_context(tc.psum_pool(name="accp", bufs=4))

        ident = const.tile([P, P], F32, name="ident", tag="ident")
        make_identity(nc, ident[:])

        sc = const.tile([P, NG, 1, 2, 2], F32, name="sc", tag="sc")
        nc.gpsimd.dma_start(
            out=sc[:, :, 0, :, :],
            in_=wqkv_scale.rearrange("o (g p u e) -> p (o g) u e", p=P, u=2, e=2),
        )
        cosb = const.tile([P, 4, 64], BF16, name="cosb", tag="cosb")
        sinb = const.tile([P, 4, 64], BF16, name="sinb", tag="sinb")

        w_par = wqkv_bytes.rearrange("(j q) k -> q j k", q=2)

        def w_rows(t, a):
            if t < 5:
                return w_par[a // 2, 256 * t + 128 * (a % 2) : 256 * t + 128 * (a % 2) + 128, :]
            return wqkv_bytes[2560 + 128 * a : 2560 + 128 * a + 128, :]

        wbytes = {}

        def load_w(t, a):
            wb = wbp.tile([P, D], U8, name="wbytes", tag="wbytes")
            nc.sync.dma_start(out=wb[:], in_=w_rows(t, a))
            wbytes[(t, a)] = wb

        xs = {}

        def load_x(m):
            xt = xp.tile([P, D], BF16, name="xs", tag="xs")
            nc.sync.dma_start(out=xt[:], in_=x[128 * m : 128 * m + 128, :])
            xs[m] = xt

        for a in range(4):
            load_w(0, a)
        load_w(1, 0)
        load_w(1, 1)
        nc.sync.dma_start(out=cosb[:], in_=freqs_cos.rearrange("(m p) i -> p m i", p=P))
        nc.sync.dma_start(out=sinb[:], in_=freqs_sin.rearrange("(m p) i -> p m i", p=P))
        for m in range(4):
            load_x(m)
        for t in range(1, NT):
            for a in range(4):
                if (t, a) not in ((1, 0), (1, 1)):
                    load_w(t, a)

        tab = const.tile([P, 4, 2, 1, 64, 2], BF16, name="tab", tag="tab")

        def tables():
            for q, f, src, sign in ((0, 0, cosb, 1.0), (0, 1, sinb, -1.0), (1, 0, sinb, 1.0), (1, 1, cosb, 1.0)):
                nc.gpsimd.tensor_scalar(out=tab[:, :, f, 0, :, q], in0=src[:], scalar1=sign, scalar2=0.0, op0=MULT, op1=ADD)

        ctx.enter_context(tc.manual_schedule())

        def transposes(pt, words, w0):
            for u in range(2):
                for b in range(2):
                    nc.tensor.transpose(
                        out=pt[:, u, 128 * b : 128 * b + 128],
                        in_=words[b][:, w0 + u : w0 + 256 : 2],
                        identity=ident[:],
                    )

        def new_gr(h):
            return grp.tile([P, 2, 512, 4], BF16, name="gr%d" % h, tag="gr%d" % h, align_bytes=64)

        def new_bank():
            return ptp.tile([P, 2, 256], F32, name="pt", tag="pt")

        wf = {}
        pts = {}
        tmps = {}
        gr = {}
        wc = {}
        accs = {}
        prs = {}

        def ok(t):
            return 0 <= t < NT

        def widen(t, a, by_vector=False):
            if not ok(t):
                return
            w16 = wfp.tile([P, D], BF16, name="wf", tag="wf")
            if by_vector:
                nc.vector.tensor_copy(out=w16[:], in_=wbytes[(t, a)][:].bitcast(FP8))
            else:
                nc.scalar.copy(out=w16[:], in_=wbytes[(t, a)][:].bitcast(FP8))
            wf[(t, a)] = w16

        def lane(t, unit):
            if unit in HELPED:
                return LANES[t][HELPED.index(unit)]
            return MORE_LANES.get((t, unit[0], unit[1]), "V")

        def trans(t, unit):
            if not ok(t):
                return
            pr, g = unit
            ww = [wf[(t, 2 * pr)][:].bitcast(F32), wf[(t, 2 * pr + 1)][:].bitcast(F32)]
            pt = new_bank()
            transposes(pt, ww, 256 * g)
            pts[(t, unit)] = pt

        def dst_of(t, unit):
            pr, g = unit
            if (t, g // 2) not in gr:
                gr[(t, g // 2)] = new_gr(g // 2)
            return gr[(t, g // 2)][:, g % 2, 256 * pr : 256 * pr + 256, :]

        def evac_s(t, unit):
            if not ok(t) or lane(t, unit) == "V":
                return
            g = unit[1]
            pt = pts[(t, unit)]
            if lane(t, unit) == "S":
                planes = pt[:].bitcast(BF16).rearrange("p u (r e) -> p u e r", e=2)
                dst = dst_of(t, unit)
                for u in range(2):
                    for e in range(2):
                        nc.scalar.activation(
                            out=dst[:, :, 2 * u + e],
                            in_=planes[:, u, e, :],
                            func=COPY,
                            scale=sc[:, g, 0, u, e : e + 1],
                        )
                return
            if lane(t, unit) in ("Y", "H", "T"):
                r0 = 128 if lane(t, unit) == "H" else 0
                if lane(t, unit) == "T":
                    tmp = tmqp.tile([P, 4, 256], BF16, name="tmq", tag="tmq")
                else:
                    tmp = tmpp.tile([P, 4, 256], BF16, name="tmp", tag="tmp")
                planes = pt[:].bitcast(BF16).rearrange("p u (r e) -> p u e r", e=2)
                for u in range(2):
                    for e in range(2):
                        nc.scalar.activation(
                            out=tmp[:, 2 * u + e, r0:256],
                            in_=planes[:, u, e, r0:256],
                            func=COPY,
                            scale=sc[:, g, 0, u, e : e + 1],
                        )
                if lane(t, unit) == "T":
                    nc.scalar.copy(out=dst_of(t, unit), in_=tmp[:].rearrange("p t r -> p r t"))
                    return
            else:
                tmp = tmpp.tile([P, 256, 4], BF16, name="tmp", tag="tmp")
                nc.scalar.copy(
                    out=tmp[:].rearrange("p r t -> p (r t)").bitcast(F32).rearrange("p (r u) -> p r u", u=2),
                    in_=pt[:].rearrange("p u r -> p r u"),
                )
            tmps[(t, unit)] = tmp

        def unit_v(t, unit):
            if not ok(t) or lane(t, unit) not in ("V", "H"):
                return
            g = unit[1]
            rows = 128 if lane(t, unit) == "H" else 256
            nc.vector.tensor_tensor(
                out=dst_of(t, unit)[:, 0:rows, :].rearrange("p r (u e) -> p r u e", u=2),
                in0=pts[(t, unit)][:].bitcast(BF16).rearrange("p u (r e) -> p r u e", e=2)[:, 0:rows, :, :],
                in1=sc[:, g, :, :, :].to_broadcast([P, rows, 2, 2]),
                op=MULT,
            )

        def unit_g(t, unit):
            if not ok(t) or lane(t, unit) in ("V", "S", "T"):
                return
            g = unit[1]
            if lane(t, unit) in ("Y", "H"):
                r0 = 128 if lane(t, unit) == "H" else 0
                nc.gpsimd.tensor_scalar(
                    out=dst_of(t, unit)[:, r0:256, :],
                    in0=tmps[(t, unit)][:, :, r0:256].rearrange("p t r -> p r t"),
                    scalar1=1.0,
                    scalar2=0.0,
                    op0=MULT,
                    op1=ADD,
                )
            else:
                nc.gpsimd.tensor_tensor(
                    out=dst_of(t, unit).rearrange("p r (u e) -> p r u e", u=2),
                    in0=tmps[(t, unit)][:].rearrange("p r (u e) -> p r u e", u=2),
                    in1=sc[:, g, :, :, :].to_broadcast([P, 256, 2, 2]),
                    op=MULT,
                )

        def quant(t, g0, n):
            if t not in wc:
                wct = wcp.tile([P, NG, 512], U32, name="wc", tag="wc", align_bytes=64)
                wst = wcp.tile([P, NG, 512], U8, name="wsc", tag="wsc", align_bytes=64)
                wc[t] = (wct, wst)
            wct, wst = wc[t]
            nc.vector.quantize_mx(
                out=wct[:, g0 : g0 + n, :].rearrange("p g n -> p (g n)").bitcast(FP8X4),
                scales=wst[:, g0 : g0 + n, :].rearrange("p g n -> p (g n)"),
                in_=gr[(t, g0 // 2)][:, g0 % 2 : g0 % 2 + n, :, :].rearrange("p g r t -> p (g r t)"),
            )

        q_flat = out_0.rearrange("s h d -> s (h d)")
        k_flat = out_1.rearrange("s h d -> s (h d)")
        v_flat = out_2.rearrange("s h d -> s (h d)")

        def mm(t, passes, first, last, tiles=(0, 1, 2, 3)):
            wct, wst = wc[t]
            for m in tiles:
                if first and t == NT - 1 and m >= 2:
                    acc = ptp.tile([P, 512, 1], F32, name="pt", tag="pt")
                    accs[(t, m)] = acc
                elif first:
                    acc = accp.tile([P, 512, 1], F32, name="acc", tag="acc")
                    accs[(t, m)] = acc
                for g in passes:
                    nc.tensor.matmul_mx(
                        out=accs[(t, m)][:, :, 0],
                        lhsT=xc[:, g, 128 * m : 128 * m + 128].bitcast(FP8X4),
                        lhsT_scale=xsc[:, g, 128 * m : 128 * m + 128],
                        rhs=wct[:, g, :].bitcast(FP8X4),
                        rhs_scale=wst[:, g, :],
                        start=(first and g == passes[0]),
                        stop=(last and g == passes[-1]),
                    )

        def rope_v(t, m):
            if not ok(t):
                return
            pr = prp.tile([P, 512, 2], F32, name="pr", tag="pr")
            nc.vector.tensor_tensor(
                out=pr[:].rearrange("p (f h i) q -> p f h i q", f=2, h=4),
                in0=accs[(t, m)][:].rearrange("p (f h i) o -> p f h i o", f=2, h=4).to_broadcast([P, 2, 4, 64, 2]),
                in1=tab[:, m, :, :, :, :].to_broadcast([P, 2, 4, 64, 2]),
                op=MULT,
            )
            prs[(t, m)] = pr

        def add_g(t, m):
            if not ok(t):
                return
            o = op.tile([P, 512], F32, name="o", tag="o")
            pr = prs[(t, m)][:].rearrange("p n q -> p (n q)")
            nc.gpsimd.tensor_tensor(out=o[:], in0=pr[:, 0:512], in1=pr[:, 512:1024], op=ADD)
            rows = slice(128 * m, 128 * m + 128)
            if t < 4:
                nc.sync.dma_start(out=q_flat[rows, 512 * t : 512 * t + 512], in_=o[:])
            else:
                nc.sync.dma_start(out=k_flat[rows, :], in_=o[:])

        def copy_out(m):
            o = op.tile([P, 512], F32, name="o", tag="o")
            if m % 2 == 0:
                nc.scalar.copy(out=o[:], in_=accs[(NT - 1, m)][:, :, 0])
                nc.scalar.dma_start(out=v_flat[128 * m : 128 * m + 128, :], in_=o[:])
            else:
                nc.vector.tensor_copy(out=o[:], in_=accs[(NT - 1, m)][:, :, 0])
                nc.sync.dma_start(out=v_flat[128 * m : 128 * m + 128, :], in_=o[:])

        xc = const.tile([P, NG, S], U32, name="xc", tag="xc", align_bytes=64)
        xsc = const.tile([P, NG, S], U8, name="xsc", tag="xsc", align_bytes=64)
        xg = [
            const.tile([P, 2, 512, 4], BF16, name="xg0", tag="xg0", align_bytes=64),
            const.tile([P, 2, 512, 4], BF16, name="xg1", tag="xg1", align_bytes=64),
        ]

        def x_unit(pr, g):
            xw = [xs[2 * pr][:].bitcast(F32), xs[2 * pr + 1][:].bitcast(F32)]
            pt = accp.tile([P, 2, 256], F32, name="acc", tag="acc")
            transposes(pt, xw, 256 * g)
            nc.scalar.copy(
                out=xg[g // 2][:, g % 2, :, :]
                .rearrange("p r t -> p (r t)")[:, 1024 * pr : 1024 * pr + 1024]
                .bitcast(F32)
                .rearrange("p (r u) -> p r u", u=2),
                in_=pt[:].rearrange("p u r -> p r u"),
            )

        def quant_x(h):
            nc.vector.quantize_mx(
                out=xc[:, 2 * h : 2 * h + 2, :].rearrange("p g n -> p (g n)").bitcast(FP8X4),
                scales=xsc[:, 2 * h : 2 * h + 2, :].rearrange("p g n -> p (g n)"),
                in_=xg[h][:].rearrange("p g r t -> p (g r t)"),
            )

        widen(0, 0, by_vector=True)
        widen(0, 1)
        widen(0, 2, by_vector=True)
        widen(0, 3, by_vector=True)
        widen(1, 0, by_vector=True)
        widen(1, 1)
        tables()
        trans(0, (0, 0))
        trans(0, (0, 1))
        trans(0, (0, 2))
        trans(0, (0, 3))
        unit_v(0, (0, 0))
        unit_v(0, (0, 1))
        evac_s(0, (0, 2))
        evac_s(0, (0, 3))
        trans(0, (1, 0))
        x_unit(0, 0)
        trans(0, (1, 1))
        x_unit(0, 1)
        unit_g(0, (0, 2))
        unit_v(0, (1, 0))
        trans(0, (1, 2))
        x_unit(0, 2)
        unit_g(0, (0, 3))
        unit_v(0, (1, 1))
        trans(0, (1, 3))
        x_unit(0, 3)
        for g in range(NG):
            x_unit(1, g)
        unit_v(0, (1, 2))
        unit_v(0, (1, 3))
        trans(1, (0, 2))
        evac_s(1, (0, 2))
        trans(1, (0, 3))
        evac_s(1, (0, 3))
        trans(1, (0, 0))
        widen(1, 2)
        quant(0, 0, 2)
        quant_x(0)
        mm(0, (0, 1), True, False, (0,))
        trans(1, (0, 1))
        mm(0, (0, 1), True, False, (1, 2))
        quant(0, 2, 2)
        quant_x(1)
        mm(0, (2, 3), False, True, (0, 1))

        for t in range(1, NT - 1):
            widen(t, 3)
            unit_g(t, (0, 2))
            add_g(t - 2, 3)
            unit_v(t, (0, 0))
            unit_g(t, (0, 3))
            unit_v(t, (0, 1))
            trans(t, (1, 2))
            widen(t + 1, 0)
            evac_s(t, (1, 2))
            trans(t, (1, 0))
            trans(t, (1, 1))
            trans(t, (1, 3))
            if t > 0:
                mm(t - 1, (2, 3), False, True, (2,))
            widen(t + 1, 1)
            widen(t + 1, 2)
            rope_v(t - 1, 0)
            add_g(t - 1, 0)
            rope_v(t - 1, 1)
            add_g(t - 1, 1)
            unit_g(t, (1, 2))
            unit_v(t, (1, 2))
            unit_v(t, (1, 0))
            trans(t + 1, (0, 2))
            mm(t - 1, (0, 1), True, False, (3,))
            evac_s(t + 1, (0, 2))
            rope_v(t - 1, 2)
            add_g(t - 1, 2)
            trans(t + 1, (0, 3))
            evac_s(t + 1, (0, 3))
            unit_v(t, (1, 1))
            trans(t + 1, (0, 0))
            mm(t - 1, (2, 3), False, True, (3,))
            unit_v(t, (1, 3))
            trans(t + 1, (0, 1))
            quant(t, 0, 2)
            if t == NT - 2:
                widen(t + 1, 3)
                trans(t + 1, (1, 0))
                evac_s(t + 1, (1, 0))
                trans(t + 1, (1, 1))
                evac_s(t + 1, (1, 1))
            mm(t, (0, 1), True, False, (0, 1, 2))
            rope_v(t - 1, 3)
            quant(t, 2, 2)
            mm(t, (2, 3), False, True, (0, 1))

        t = NT - 1
        unit_g(t, (0, 2))
        add_g(t - 2, 3)
        unit_v(t, (0, 0))
        unit_g(t, (0, 3))
        unit_v(t, (0, 1))
        mm(t - 1, (2, 3), False, True, (2,))
        trans(t, (1, 2))
        evac_s(t, (1, 2))
        mm(t - 1, (0, 1), True, False, (3,))
        trans(t, (1, 3))
        evac_s(t, (1, 3))
        mm(t - 1, (2, 3), False, True, (3,))
        rope_v(t - 1, 0)
        add_g(t - 1, 0)
        rope_v(t - 1, 1)
        add_g(t - 1, 1)
        quant(t, 0, 2)
        mm(t, (0, 1), True, False)
        rope_v(t - 1, 2)
        add_g(t - 1, 2)
        quant(t, 2, 1)
        mm(t, (2,), False, False)
        rope_v(t - 1, 3)
        add_g(t - 1, 3)
        quant(t, 3, 1)
        mm(t, (3,), False, True)
        for m in range(4):
            copy_out(m)
